import numpy as np
import ml_dtypes


def mxq(x, axis, fmt="e4m3"):
    dtype, down = {"e4m3": (ml_dtypes.float8_e4m3fn, 7), "e5m2": (ml_dtypes.float8_e5m2, 14)}[fmt]
    v = np.moveaxis(np.asarray(x, np.float32).astype(ml_dtypes.bfloat16).astype(np.float64), axis, -1)
    blocks = v.reshape(v.shape[:-1] + (-1, 32))
    amax = np.abs(blocks).max(-1, keepdims=True)
    byte = np.maximum(np.where(amax > 0, np.frexp(amax)[1] - 1 + 127, 0) - down, 1)
    scale = np.exp2(byte - 127.0)
    codes = (blocks / scale).astype(np.float32).astype(dtype).astype(np.float64)
    return np.moveaxis((codes * scale).reshape(v.shape), -1, axis)


WIDE = False


def mx_kscale(k):
    if not WIDE:
        return np.ones(k)
    levels = np.array([10, -10, 5, -5, 0])
    a = np.random.permutation(np.resize(levels, k // 512 * 4)).reshape(k // 512, 4)
    idx = np.arange(k)
    return np.exp2(a[idx // 512, idx % 128 // 32])


BF16 = ml_dtypes.bfloat16


def bf(x):
    return np.asarray(x, np.float32).astype(BF16)


def f64(x):
    return np.asarray(x).astype(np.float64)


T, B, E, H, K = 1024, 2, 1024, 16, 16
R = E // H
PAD_L = K // 2


def softmax_last(z):
    e = np.exp(z - z.max(-1, keepdims=True))
    return e / e.sum(-1, keepdims=True)


def setup_inputs():
    a, s = mx_kscale(E), mx_kscale(E)
    return {
        "v": bf(np.random.standard_normal((T, B, E)) * s),
        "attn_out": bf(np.random.standard_normal((T, B, E)) * 0.3 * a),
        "dyn_w": bf(np.random.standard_normal((H * K, E)) / np.sqrt(E) / s),
        "dyn_b": bf(np.random.standard_normal(H * K) * 0.1),
        "out_proj_w": bf(np.random.standard_normal((E, 2 * E)) * 1.5 / np.sqrt(E) / np.concatenate([a, s])),
        "out_proj_b": bf(np.random.standard_normal(E) * 0.1),
    }


def reference(v, attn_out, dyn_w, dyn_b, out_proj_w, out_proj_b):
    v = f64(v)
    logits = (mxq(v, 2, "e4m3") @ mxq(f64(dyn_w), 1, "e4m3").T) + f64(dyn_b)
    w = softmax_last(logits.reshape(T, B, H, K))
    xh = np.pad(v, ((PAD_L, K - 1 - PAD_L), (0, 0), (0, 0))).reshape(T + K - 1, B, H, R)
    conv = np.zeros((T, B, H, R))
    for k in range(K):
        conv = conv + w[..., k:k + 1] * xh[k:k + T]
    cat = np.concatenate([f64(attn_out), conv.reshape(T, B, E)], axis=-1)
    return (mxq(cat, 2, "e4m3") @ mxq(f64(out_proj_w), 1, "e4m3").T) + f64(out_proj_b)

@@ -1,0 +1,356 @@
+from contextlib import ExitStack
+
+import concourse.mybir as mybir
+from concourse.masks import make_identity
+
+F32 = mybir.dt.float32
+BF16 = mybir.dt.bfloat16
+U32 = mybir.dt.uint32
+U8 = mybir.dt.uint8
+FP8X4 = mybir.dt.float8_e4m3fn_x4
+ALU = mybir.AluOpType
+ACT = mybir.ActivationFunctionType
+AXIS = mybir.AxisListType
+
+T, B, E, H, TAPS = 1024, 2, 1024, 16, 16
+R = E // H
+PAD_L = TAPS // 2
+HK = H * TAPS
+
+P = 128
+PACK = 4
+K_PASS = P * PACK
+WORDS = E // 2
+UNITS = 4
+ROWS = UNITS * P
+N_TILE = 512
+TOKENS = T * B
+
+WINDOW_STEP = P - TAPS
+N_WINDOWS = (T - P) // WINDOW_STEP + 1
+PHASES = 8
+
+PART = T + TAPS
+ROW_PITCH = B * PART
+HEAD_PITCH = TAPS * ROW_PITCH - TAPS
+N_GAPS = TAPS * B - 1
+
+FLOPS = 2 * TOKENS * E * HK + 2 * TOKENS * (2 * E) * E + 2 * TOKENS * E * TAPS
+
+
+def tile_multiheadattention820_pa_kernel(tc, v, attn_out, dyn_w, dyn_b, out_proj_w, out_proj_b, out):
+    nc = tc.nc
+    with ExitStack() as ctx:
+        consts = ctx.enter_context(tc.tile_pool(name="consts", bufs=1))
+        keep = ctx.enter_context(tc.tile_pool(name="keep", bufs=1))
+        raw_pool = ctx.enter_context(tc.tile_pool(name="raw", bufs=3))
+        stage = ctx.enter_context(tc.tile_pool(name="stage", bufs=2))
+        vq_pool = ctx.enter_context(tc.tile_pool(name="vq", bufs=2))
+        soft = ctx.enter_context(tc.tile_pool(name="soft", bufs=3))
+        band_pool = ctx.enter_context(tc.tile_pool(name="band", bufs=3))
+        win_pool = ctx.enter_context(tc.tile_pool(name="win", bufs=3))
+        conv_pool = ctx.enter_context(tc.tile_pool(name="conv", bufs=3))
+        out_pool = ctx.enter_context(tc.tile_pool(name="outp", bufs=3))
+        flip_psum = ctx.enter_context(tc.psum_pool(name="flip", bufs=3))
+        conv_psum = ctx.enter_context(tc.psum_pool(name="convp", bufs=3))
+        acc_psum = ctx.enter_context(tc.psum_pool(name="acc", bufs=2))
+
+        ident_f32 = consts.tile([P, P], F32)
+        make_identity(nc, ident_f32[:])
+        ident_bf16 = consts.tile([P, P], BF16)
+        make_identity(nc, ident_bf16[:])
+
+        band_mask = consts.tile([P, P], F32)
+        nc.gpsimd.memset(band_mask[:], 1.0)
+        nc.gpsimd.affine_select(
+            out=band_mask[:], in_=band_mask[:], compare_op=ALU.is_ge, fill=0.0,
+            base=PAD_L, pattern=[[-1, P]], channel_multiplier=1,
+        )
+        nc.gpsimd.affine_select(
+            out=band_mask[:], in_=band_mask[:], compare_op=ALU.is_ge, fill=0.0,
+            base=TAPS - 1 - PAD_L, pattern=[[1, P]], channel_multiplier=-1,
+        )
+
+        dyn_b_bf16 = consts.tile([P, HK], BF16)
+        nc.gpsimd.dma_start(out=dyn_b_bf16[:], in_=dyn_b.partition_broadcast(P))
+        dyn_b_f32 = consts.tile([P, HK], F32)
+        nc.vector.tensor_copy(out=dyn_b_f32[:], in_=dyn_b_bf16[:])
+        out_b_bf16 = consts.tile([P, E], BF16)
+        nc.gpsimd.dma_start(out=out_b_bf16[:], in_=out_proj_b.partition_broadcast(P))
+        out_b_f32 = consts.tile([P, E], F32)
+        nc.vector.tensor_copy(out=out_b_f32[:], in_=out_b_bf16[:])
+
+        v_by_phase = v.rearrange("(p j) b c -> p j b c", j=PHASES)
+        attn_rows = attn_out.rearrange("(n p) b c -> p n b c", p=P)
+        dyn_rows = dyn_w.rearrange("(n p) c -> p n c", p=P)
+        w_rows = out_proj_w.rearrange("(n p) c -> p n c", p=P)
+        out_rows = out.rearrange("(n p) b e -> p n b e", p=P)
+        scratch = out.rearrange("t b e -> (t b e)")
+
+        zeros = consts.tile([H, N_GAPS * TAPS], F32)
+        nc.vector.memset(zeros[:], 0.0)
+        gaps = (
+            scratch[0 : H * HEAD_PITCH]
+            .rearrange("(h z) -> h z", z=HEAD_PITCH)[:, 0 : N_GAPS * PART]
+            .rearrange("h (m y) -> h m y", y=PART)[:, :, T:PART]
+        )
+        nc.sync.dma_start(out=gaps, in_=zeros[:].rearrange("h (m y) -> h m y", y=TAPS))
+
+        d_codes = keep.tile([P, 2 * HK], U32, align_bytes=64)
+        d_scales = keep.tile([P, 2 * HK], U8, align_bytes=64)
+        w_codes = keep.tile([P, 4 * E], U32, align_bytes=64)
+        w_scales = keep.tile([P, 4 * E], U8, align_bytes=64)
+        a_codes = keep.tile([P, 2 * TOKENS], U32, align_bytes=64)
+        a_scales = keep.tile([P, 2 * TOKENS], U8, align_bytes=64)
+        c_codes = keep.tile([P, 2 * TOKENS], U32, align_bytes=64)
+        c_scales = keep.tile([P, 2 * TOKENS], U8, align_bytes=64)
+
+        def load_rows(view):
+            raw = raw_pool.tile([P, UNITS * E], BF16)
+            blocks = view.shape[1]
+            nc.scalar.dma_start(out=raw[:, 0 : blocks * E].rearrange("p (n c) -> p n c", c=E), in_=view)
+            return raw
+
+        def quantise_rows(raw, blocks, codes, scales, pass_cols):
+            words = raw[:].bitcast(F32)
+            grouped = stage.tile([P, 2 * ROWS * PACK], BF16, align_bytes=64)
+            grouped_words = grouped[:].bitcast(F32).rearrange("p (g r u) -> p g r u", g=2, u=2)
+            for n in range(blocks):
+                flipped = flip_psum.tile([P, 4 * P], F32, tag="flip")
+                for gu in range(4):
+                    first = n * WORDS + gu * P
+                    nc.tensor.transpose(flipped[:, gu * P : (gu + 1) * P], words[:, first : first + P], ident_f32[:])
+                nc.scalar.copy(
+                    out=grouped_words[:, :, n * P : (n + 1) * P, :],
+                    in_=flipped[:].rearrange("p (g u r) -> p g r u", g=2, u=2),
+                )
+            rows = blocks * P
+            for g in range(2):
+                cols = slice(pass_cols[g], pass_cols[g] + rows)
+                nc.vector.quantize_mx(
+                    out=codes[:, cols].bitcast(FP8X4),
+                    scales=scales[:, cols],
+                    in_=grouped[:, g * ROWS * PACK : g * ROWS * PACK + rows * PACK],
+                )
+
+        def softmax_over_taps(logits):
+            groups = 2 * H
+            weights = soft.tile([P, 2 * HK], F32)
+            by_head = weights[:].rearrange("p (m k) -> p m k", k=TAPS)
+            nc.vector.tensor_tensor(
+                out=weights[:].rearrange("p (n c) -> p n c", n=2),
+                in0=logits[:].rearrange("p (n c) -> p n c", n=2),
+                in1=dyn_b_f32[:].unsqueeze(1).to_broadcast([P, 2, HK]),
+                op=ALU.add,
+            )
+            top = soft.tile([P, groups], F32)
+            nc.vector.tensor_reduce(out=top[:], in_=by_head, axis=AXIS.X, op=ALU.max)
+            nc.vector.tensor_tensor(
+                out=by_head, in0=by_head, in1=top[:].unsqueeze(2).to_broadcast([P, groups, TAPS]), op=ALU.subtract
+            )
+            nc.scalar.activation(out=weights[:], in_=weights[:], func=ACT.Exp)
+            total = soft.tile([P, groups], F32)
+            nc.vector.tensor_reduce(out=total[:], in_=by_head, axis=AXIS.X, op=ALU.add)
+            inverse = soft.tile([P, groups], F32)
+            nc.vector.reciprocal(out=inverse[:], in_=total[:])
+            nc.vector.tensor_tensor(
+                out=by_head, in0=by_head, in1=inverse[:].unsqueeze(2).to_broadcast([P, groups, TAPS]), op=ALU.mult
+            )
+            return weights
+
+        raw_d = load_rows(dyn_rows)
+        quantise_rows(raw_d, 2, d_codes, d_scales, [0, HK])
+
+        skewed = {}
+
+        def logits_block(b, quad):
+            raw_v = load_rows(v_by_phase[:, quad * UNITS : (quad + 1) * UNITS, b, :])
+            v_codes = vq_pool.tile([P, 2 * ROWS], U32, align_bytes=64)
+            v_scales = vq_pool.tile([P, 2 * ROWS], U8, align_bytes=64)
+            quantise_rows(raw_v, UNITS, v_codes, v_scales, [0, ROWS])
+            for pair in range(UNITS // 2):
+                logits = acc_psum.tile([P, N_TILE], F32, tag="acc")
+                for n in range(2):
+                    for g in range(2):
+                        cols = slice(g * ROWS + (2 * pair + n) * P, g * ROWS + (2 * pair + n + 1) * P)
+                        nc.tensor.matmul_mx(
+                            out=logits[:, n * HK : (n + 1) * HK],
+                            lhsT=v_codes[:, cols].bitcast(FP8X4),
+                            lhsT_scale=v_scales[:, cols],
+                            rhs=d_codes[:, g * HK : (g + 1) * HK].bitcast(FP8X4),
+                            rhs_scale=d_scales[:, g * HK : (g + 1) * HK],
+                            start=(g == 0),
+                            stop=(g == 1),
+                        )
+                weights = softmax_over_taps(logits)
+                for n in range(2):
+                    j = quad * UNITS + 2 * pair + n
+                    for odd in range(2):
+                        first = (PHASES * odd + j) * ROW_PITCH + b * PART
+                        rows_of_i = (
+                            scratch[first : first + H * HEAD_PITCH]
+                            .rearrange("(h z) -> h z", z=HEAD_PITCH)[:, 0:T]
+                            .rearrange("h (a k) -> a h k", k=TAPS)
+                        )
+                        nc.sync.dma_start(
+                            out=rows_of_i,
+                            in_=weights[odd:P:2, n * HK : (n + 1) * HK].rearrange("a (h k) -> a h k", k=TAPS),
+                        )
+
+        def read_skewed(b):
+            for half in range(2):
+                first = half * P * (ROW_PITCH - 1) + b * PART + PAD_L
+                skew = keep.tile([P, T], F32, name="skew%d%d" % (b, half))
+                nc.sync.dma_start(
+                    out=skew[:],
+                    in_=scratch[first : first + P * (ROW_PITCH - 1)].rearrange("(p y) -> p y", y=ROW_PITCH - 1)[:, 0:T],
+                )
+                skewed[(b, half)] = skew
+
+        for quad in range(PHASES // UNITS):
+            logits_block(0, quad)
+        read_skewed(0)
+
+        for nh in range(E // N_TILE):
+            for part in range(2):
+                raw_w = load_rows(w_rows[:, nh * UNITS : (nh + 1) * UNITS, part * E : (part + 1) * E])
+                quantise_rows(
+                    raw_w, UNITS, w_codes, w_scales,
+                    [(2 * part) * E + nh * N_TILE, (2 * part + 1) * E + nh * N_TILE],
+                )
+        for b in range(B):
+            for quad in range(T // ROWS):
+                raw_a = load_rows(attn_rows[:, quad * UNITS : (quad + 1) * UNITS, b, :])
+                col0 = b * T + quad * ROWS
+                quantise_rows(raw_a, UNITS, a_codes, a_scales, [col0, TOKENS + col0])
+
+        def project(b, block):
+            tok = b * T + block * P
+            result = out_pool.tile([P, E], F32)
+            for nh in range(E // N_TILE):
+                acc = acc_psum.tile([P, N_TILE], F32, tag="acc")
+                for c in range(4):
+                    codes, scales = (a_codes, a_scales) if c < 2 else (c_codes, c_scales)
+                    cols = slice((c % 2) * TOKENS + tok, (c % 2) * TOKENS + tok + P)
+                    outs = slice(c * E + nh * N_TILE, c * E + (nh + 1) * N_TILE)
+                    nc.tensor.matmul_mx(
+                        out=acc[:],
+                        lhsT=codes[:, cols].bitcast(FP8X4),
+                        lhsT_scale=scales[:, cols],
+                        rhs=w_codes[:, outs].bitcast(FP8X4),
+                        rhs_scale=w_scales[:, outs],
+                        start=(c == 0),
+                        stop=(c == 3),
+                    )
+                nc.vector.tensor_tensor(
+                    out=result[:, nh * N_TILE : (nh + 1) * N_TILE],
+                    in0=acc[:],
+                    in1=out_b_f32[:, nh * N_TILE : (nh + 1) * N_TILE],
+                    op=ALU.add,
+                )
+            nc.sync.dma_start(out=out_rows[:, block, b, :], in_=result[:])
+
+        steps = []
+        for b in range(B):
+            for w in range(N_WINDOWS):
+                steps.append((b, w))
+        windows = {}
+        bands = {}
+        conv_tiles = {}
+        conv_groups = {}
+        finished = {}
+
+        def fetch_window(s):
+            b, w = steps[s]
+            t0 = w * WINDOW_STEP
+            window_bf16 = win_pool.tile([P, E], BF16)
+            nc.sync.dma_start(out=window_bf16[:], in_=v[t0 : t0 + P, b, :])
+            window = win_pool.tile([P, E], F32)
+            nc.gpsimd.tensor_scalar(
+                out=window[:], in0=window_bf16[:], scalar1=1.0, scalar2=0.0, op0=ALU.mult, op1=ALU.add
+            )
+            windows[s] = window
+
+        def make_band(s):
+            b, w = steps[s]
+            t0 = w * WINDOW_STEP
+            by_time = flip_psum.tile([P, HK], F32, tag="flip")
+            for half in range(2):
+                nc.tensor.transpose(
+                    by_time[:, half * P : (half + 1) * P], skewed[(b, half)][:, t0 : t0 + P], ident_f32[:]
+                )
+            band = band_pool.tile([P, H * P], F32)
+            nc.vector.tensor_tensor(
+                out=band[:].rearrange("p (h a i) -> p h a i", h=H, i=TAPS),
+                in0=by_time[:].rearrange("p (h i) -> p h i", i=TAPS).unsqueeze(2).to_broadcast([P, H, P // TAPS, TAPS]),
+                in1=band_mask[:].rearrange("p (a i) -> p a i", i=TAPS).unsqueeze(1).to_broadcast([P, H, P // TAPS, TAPS]),
+                op=ALU.mult,
+            )
+            bands[s] = band
+
+        def convolve(s):
+            conv_bf16 = conv_pool.tile([P, E], BF16)
+            for g in range(2):
+                conv_f32 = conv_psum.tile([P, K_PASS], F32, tag="conv")
+                for hl in range(K_PASS // R):
+                    h = g * (K_PASS // R) + hl
+                    nc.tensor.matmul(
+                        out=conv_f32[:, hl * R : (hl + 1) * R],
+                        lhsT=bands[s][:, h * P : (h + 1) * P],
+                        rhs=windows[s][:, h * R : (h + 1) * R],
+                        start=True,
+                        stop=True,
+                    )
+                nc.scalar.copy(
+                    out=conv_bf16[:, g * K_PASS : (g + 1) * K_PASS].rearrange("x (u e q) -> x u e q", u=2, e=2),
+                    in_=conv_f32[:].rearrange("x (u q e) -> x u e q", u=2, e=2),
+                )
+            conv_tiles[s] = conv_bf16
+
+        def flip_conv(s):
+            b, w = steps[s]
+            t0 = w * WINDOW_STEP
+            if w == 0:
+                grouped_conv = keep.tile([P, 2 * T * PACK], BF16, align_bytes=64)
+                conv_groups[b] = grouped_conv
+            flipped_conv = flip_psum.tile([P, 2 * PACK * P], BF16, tag="flip")
+            for n in range(2 * PACK):
+                nc.tensor.transpose(
+                    flipped_conv[:, n * P : (n + 1) * P], conv_tiles[s][:, n * P : (n + 1) * P], ident_bf16[:]
+                )
+            lo = 0 if w == 0 else PAD_L
+            hi = P if w == N_WINDOWS - 1 else P - PAD_L
+            nc.scalar.copy(
+                out=conv_groups[b][:].rearrange("p (g n t) -> p g n t", g=2, t=PACK)[:, :, t0 + lo : t0 + hi, :],
+                in_=flipped_conv[:].rearrange("p (g t x) -> p g x t", g=2, t=PACK)[:, :, lo:hi, :],
+            )
+            first_block = 0 if w == 0 else (t0 - WINDOW_STEP + P - PAD_L) // P
+            finished[s] = []
+            for block in range(first_block, (t0 + hi) // P):
+                tok = b * T + block * P
+                for g in range(2):
+                    first = (g * T + block * P) * PACK
+                    nc.vector.quantize_mx(
+                        out=c_codes[:, g * TOKENS + tok : g * TOKENS + tok + P].bitcast(FP8X4),
+                        scales=c_scales[:, g * TOKENS + tok : g * TOKENS + tok + P],
+                        in_=conv_groups[b][:, first : first + P * PACK],
+                    )
+                finished[s].append(block)
+
+        n_steps = len(steps)
+        for r in range(n_steps + 4):
+            if r >= 4:
+                for block in finished[r - 4]:
+                    project(steps[r - 4][0], block)
+            if 2 <= r < n_steps + 2:
+                convolve(r - 2)
+            if 3 <= r < n_steps + 3:
+                flip_conv(r - 3)
+            if 1 <= r < n_steps + 1:
+                make_band(r - 1)
+            if r < n_steps:
+                fetch_window(r)
+            if r < PHASES // UNITS:
+                logits_block(1, r)
+            if r == PHASES // UNITS:
+                read_skewed(1)

@@ -35,6 +35,8 @@ ROW_PITCH = B * PART
 HEAD_PITCH = TAPS * ROW_PITCH - TAPS
 N_GAPS = TAPS * B - 1
 
+HEADS_PER_PASS = K_PASS // R
+
 FLOPS = 2 * TOKENS * E * HK + 2 * TOKENS * (2 * E) * E + 2 * TOKENS * E * TAPS
 
 
@@ -70,6 +72,9 @@ def tile_multiheadattention820_pa_kernel(tc, v, attn_out, dyn_w, dyn_b, out_proj
             out=band_mask[:], in_=band_mask[:], compare_op=ALU.is_ge, fill=0.0,
             base=TAPS - 1 - PAD_L, pattern=[[1, P]], channel_multiplier=-1,
         )
+
+        band_mask_bf16 = consts.tile([P, P], BF16)
+        nc.vector.tensor_copy(out=band_mask_bf16[:], in_=band_mask[:])
 
         dyn_b_bf16 = consts.tile([P, HK], BF16)
         nc.gpsimd.dma_start(out=dyn_b_bf16[:], in_=dyn_b.partition_broadcast(P))
@@ -265,11 +270,18 @@ def tile_multiheadattention820_pa_kernel(tc, v, attn_out, dyn_w, dyn_b, out_proj
             t0 = w * WINDOW_STEP
             window_bf16 = win_pool.tile([P, E], BF16)
             nc.sync.dma_start(out=window_bf16[:], in_=v[t0 : t0 + P, b, :])
-            window = win_pool.tile([P, E], F32)
+            window_f32 = win_pool.tile([P, K_PASS], F32)
             nc.gpsimd.tensor_scalar(
-                out=window[:], in0=window_bf16[:], scalar1=1.0, scalar2=0.0, op0=ALU.mult, op1=ALU.add
+                out=window_f32[:], in0=window_bf16[:, K_PASS:E], scalar1=1.0, scalar2=0.0, op0=ALU.mult, op1=ALU.add
             )
-            windows[s] = window
+            windows[s] = (window_bf16, window_f32)
+
+        def spread(taps, mask):
+            shape = [P, HEADS_PER_PASS, P // TAPS, TAPS]
+            return (
+                taps.rearrange("p (h i) -> p h i", i=TAPS).unsqueeze(2).to_broadcast(shape),
+                mask.rearrange("p (a i) -> p a i", i=TAPS).unsqueeze(1).to_broadcast(shape),
+            )
 
         def make_band(s):
             b, w = steps[s]
@@ -279,28 +291,43 @@ def tile_multiheadattention820_pa_kernel(tc, v, attn_out, dyn_w, dyn_b, out_proj
                 nc.tensor.transpose(
                     by_time[:, half * P : (half + 1) * P], skewed[(b, half)][:, t0 : t0 + P], ident_f32[:]
                 )
-            band = band_pool.tile([P, H * P], F32)
+            taps_hi = band_pool.tile([P, P], BF16)
+            nc.scalar.copy(out=taps_hi[:], in_=by_time[:, 0:P])
+            taps_lo = band_pool.tile([P, P], BF16)
+            nc.vector.tensor_tensor(out=taps_lo[:], in0=by_time[:, 0:P], in1=taps_hi[:], op=ALU.subtract)
+            band_hi = band_pool.tile([P, HEADS_PER_PASS * P], BF16)
+            in0, in1 = spread(taps_hi[:], band_mask_bf16[:])
             nc.vector.tensor_tensor(
-                out=band[:].rearrange("p (h a i) -> p h a i", h=H, i=TAPS),
-                in0=by_time[:].rearrange("p (h i) -> p h i", i=TAPS).unsqueeze(2).to_broadcast([P, H, P // TAPS, TAPS]),
-                in1=band_mask[:].rearrange("p (a i) -> p a i", i=TAPS).unsqueeze(1).to_broadcast([P, H, P // TAPS, TAPS]),
-                op=ALU.mult,
+                out=band_hi[:].rearrange("p (h a i) -> p h a i", h=HEADS_PER_PASS, i=TAPS), in0=in0, in1=in1, op=ALU.mult
             )
-            bands[s] = band
+            band_lo = band_pool.tile([P, HEADS_PER_PASS * P], BF16)
+            in0, in1 = spread(taps_lo[:], band_mask_bf16[:])
+            nc.gpsimd.tensor_tensor(
+                out=band_lo[:].rearrange("p (h a i) -> p h a i", h=HEADS_PER_PASS, i=TAPS), in0=in0, in1=in1, op=ALU.mult
+            )
+            band_f32 = band_pool.tile([P, HEADS_PER_PASS * P], F32)
+            in0, in1 = spread(by_time[:, P : 2 * P], band_mask[:])
+            nc.vector.tensor_tensor(
+                out=band_f32[:].rearrange("p (h a i) -> p h a i", h=HEADS_PER_PASS, i=TAPS), in0=in0, in1=in1, op=ALU.mult
+            )
+            bands[s] = (band_hi, band_lo, band_f32)
 
         def convolve(s):
+            window_bf16, window_f32 = windows[s]
+            band_hi, band_lo, band_f32 = bands[s]
             conv_bf16 = conv_pool.tile([P, E], BF16)
             for g in range(2):
                 conv_f32 = conv_psum.tile([P, K_PASS], F32, tag="conv")
-                for hl in range(K_PASS // R):
-                    h = g * (K_PASS // R) + hl
-                    nc.tensor.matmul(
-                        out=conv_f32[:, hl * R : (hl + 1) * R],
-                        lhsT=bands[s][:, h * P : (h + 1) * P],
-                        rhs=windows[s][:, h * R : (h + 1) * R],
-                        start=True,
-                        stop=True,
-                    )
+                for h in range(HEADS_PER_PASS):
+                    sums = conv_f32[:, h * R : (h + 1) * R]
+                    one = slice(h * P, (h + 1) * P)
+                    if g == 0:
+                        moving = window_bf16[:, h * R : (h + 1) * R]
+                        nc.tensor.matmul(out=sums, lhsT=band_hi[:, one], rhs=moving, start=True, stop=False)
+                        nc.tensor.matmul(out=sums, lhsT=band_lo[:, one], rhs=moving, start=False, stop=True)
+                    else:
+                        moving = window_f32[:, h * R : (h + 1) * R]
+                        nc.tensor.matmul(out=sums, lhsT=band_f32[:, one], rhs=moving, start=True, stop=True)
                 nc.scalar.copy(
                     out=conv_bf16[:, g * K_PASS : (g + 1) * K_PASS].rearrange("x (u e q) -> x u e q", u=2, e=2),
                     in_=conv_f32[:].rearrange("x (u q e) -> x u e q", u=2, e=2),
@@ -325,8 +352,11 @@ def tile_multiheadattention820_pa_kernel(tc, v, attn_out, dyn_w, dyn_b, out_proj
                 in_=flipped_conv[:].rearrange("p (g t x) -> p g x t", g=2, t=PACK)[:, :, lo:hi, :],
             )
             first_block = 0 if w == 0 else (t0 - WINDOW_STEP + P - PAD_L) // P
-            finished[s] = []
-            for block in range(first_block, (t0 + hi) // P):
+            finished[s] = list(range(first_block, (t0 + hi) // P))
+
+        def quantise_conv(s):
+            b = steps[s][0]
+            for block in finished[s]:
                 tok = b * T + block * P
                 for g in range(2):
                     first = (g * T + block * P) * PACK
@@ -335,19 +365,20 @@ def tile_multiheadattention820_pa_kernel(tc, v, attn_out, dyn_w, dyn_b, out_proj
                         scales=c_scales[:, g * TOKENS + tok : g * TOKENS + tok + P],
                         in_=conv_groups[b][:, first : first + P * PACK],
                     )
-                finished[s].append(block)
 
         n_steps = len(steps)
-        for r in range(n_steps + 4):
-            if r >= 4:
-                for block in finished[r - 4]:
-                    project(steps[r - 4][0], block)
+        for r in range(n_steps + 5):
+            if 1 <= r < n_steps + 1:
+                make_band(r - 1)
+            if r >= 5:
+                for block in finished[r - 5]:
+                    project(steps[r - 5][0], block)
+            if 4 <= r < n_steps + 4:
+                quantise_conv(r - 4)
             if 2 <= r < n_steps + 2:
                 convolve(r - 2)
             if 3 <= r < n_steps + 3:
                 flip_conv(r - 3)
-            if 1 <= r < n_steps + 1:
-                make_band(r - 1)
             if r < n_steps:
                 fetch_window(r)
             if r < PHASES // UNITS:

@@ -28,12 +28,15 @@ TOKENS = T * B
 
 WINDOW_STEP = P - TAPS
 N_WINDOWS = (T - P) // WINDOW_STEP + 1
-PHASES = 8
+CHUNK = UNITS * P
+CHUNKS = T // CHUNK
+ROUNDS_PER_CHUNK = 4
 
 PART = T + TAPS
 ROW_PITCH = B * PART
 HEAD_PITCH = TAPS * ROW_PITCH - TAPS
 N_GAPS = TAPS * B - 1
+SCRATCH_ROWS = 552
 
 HEADS_PER_PASS = K_PASS // R
 
@@ -85,12 +88,12 @@ def tile_multiheadattention820_pa_kernel(tc, v, attn_out, dyn_w, dyn_b, out_proj
         out_b_f32 = consts.tile([P, E], F32)
         nc.vector.tensor_copy(out=out_b_f32[:], in_=out_b_bf16[:])
 
-        v_by_phase = v.rearrange("(p j) b c -> p j b c", j=PHASES)
+        v_chunks = v.rearrange("(c p j) b e -> p c j b e", c=CHUNKS, j=UNITS)
         attn_rows = attn_out.rearrange("(n p) b c -> p n b c", p=P)
         dyn_rows = dyn_w.rearrange("(n p) c -> p n c", p=P)
         w_rows = out_proj_w.rearrange("(n p) c -> p n c", p=P)
         out_rows = out.rearrange("(n p) b e -> p n b e", p=P)
-        scratch = out.rearrange("t b e -> (t b e)")
+        scratch = out.rearrange("t b e -> (t b e)")[(TOKENS - SCRATCH_ROWS) * E : TOKENS * E]
 
         zeros = consts.tile([H, N_GAPS * TAPS], F32)
         nc.vector.memset(zeros[:], 0.0)
@@ -125,7 +128,8 @@ def tile_multiheadattention820_pa_kernel(tc, v, attn_out, dyn_w, dyn_b, out_proj
                 for gu in range(4):
                     first = n * WORDS + gu * P
                     nc.tensor.transpose(flipped[:, gu * P : (gu + 1) * P], words[:, first : first + P], ident_f32[:])
-                nc.scalar.copy(
+                copy_out = nc.vector.tensor_copy if n % UNITS == 2 else nc.scalar.copy
+                copy_out(
                     out=grouped_words[:, :, n * P : (n + 1) * P, :],
                     in_=flipped[:].rearrange("p (g u r) -> p g r u", g=2, u=2),
                 )
@@ -168,8 +172,8 @@ def tile_multiheadattention820_pa_kernel(tc, v, attn_out, dyn_w, dyn_b, out_proj
 
         skewed = {}
 
-        def logits_block(b, quad):
-            raw_v = load_rows(v_by_phase[:, quad * UNITS : (quad + 1) * UNITS, b, :])
+        def logits_chunk(b, chunk):
+            raw_v = load_rows(v_chunks[:, chunk, :, b, :])
             v_codes = vq_pool.tile([P, 2 * ROWS], U32, align_bytes=64)
             v_scales = vq_pool.tile([P, 2 * ROWS], U8, align_bytes=64)
             quantise_rows(raw_v, UNITS, v_codes, v_scales, [0, ROWS])
@@ -189,32 +193,34 @@ def tile_multiheadattention820_pa_kernel(tc, v, attn_out, dyn_w, dyn_b, out_proj
                         )
                 weights = softmax_over_taps(logits)
                 for n in range(2):
-                    j = quad * UNITS + 2 * pair + n
-                    for odd in range(2):
-                        first = (PHASES * odd + j) * ROW_PITCH + b * PART
+                    j = 2 * pair + n
+                    for m in range(TAPS // UNITS):
+                        first = (UNITS * m + j) * ROW_PITCH + b * PART + chunk * CHUNK
                         rows_of_i = (
                             scratch[first : first + H * HEAD_PITCH]
-                            .rearrange("(h z) -> h z", z=HEAD_PITCH)[:, 0:T]
+                            .rearrange("(h z) -> h z", z=HEAD_PITCH)[:, 0:CHUNK]
                             .rearrange("h (a k) -> a h k", k=TAPS)
                         )
                         nc.sync.dma_start(
                             out=rows_of_i,
-                            in_=weights[odd:P:2, n * HK : (n + 1) * HK].rearrange("a (h k) -> a h k", k=TAPS),
+                            in_=weights[m : P : TAPS // UNITS, n * HK : (n + 1) * HK].rearrange("a (h k) -> a h k", k=TAPS),
                         )
 
-        def read_skewed(b):
+        def read_skewed(b, chunk):
+            lo = 0 if chunk == 0 else chunk * CHUNK - PAD_L
+            hi = T if chunk == CHUNKS - 1 else (chunk + 1) * CHUNK - PAD_L
             for half in range(2):
+                if chunk == 0:
+                    skew = keep.tile([P, T], F32, name="skew%d%d" % (b, half))
+                    skewed[(b, half)] = skew
                 first = half * P * (ROW_PITCH - 1) + b * PART + PAD_L
-                skew = keep.tile([P, T], F32, name="skew%d%d" % (b, half))
                 nc.sync.dma_start(
-                    out=skew[:],
-                    in_=scratch[first : first + P * (ROW_PITCH - 1)].rearrange("(p y) -> p y", y=ROW_PITCH - 1)[:, 0:T],
+                    out=skewed[(b, half)][:, lo:hi],
+                    in_=scratch[first : first + P * (ROW_PITCH - 1)].rearrange("(p y) -> p y", y=ROW_PITCH - 1)[:, lo:hi],
                 )
-                skewed[(b, half)] = skew
 
-        for quad in range(PHASES // UNITS):
-            logits_block(0, quad)
-        read_skewed(0)
+        logits_chunk(0, 0)
+        read_skewed(0, 0)
 
         for nh in range(E // N_TILE):
             for part in range(2):
@@ -223,11 +229,15 @@ def tile_multiheadattention820_pa_kernel(tc, v, attn_out, dyn_w, dyn_b, out_proj
                     raw_w, UNITS, w_codes, w_scales,
                     [(2 * part) * E + nh * N_TILE, (2 * part + 1) * E + nh * N_TILE],
                 )
+
+        def quantise_attn(b, chunk):
+            raw_a = load_rows(attn_rows[:, chunk * UNITS : (chunk + 1) * UNITS, b, :])
+            col0 = b * T + chunk * CHUNK
+            quantise_rows(raw_a, UNITS, a_codes, a_scales, [col0, TOKENS + col0])
+
         for b in range(B):
-            for quad in range(T // ROWS):
-                raw_a = load_rows(attn_rows[:, quad * UNITS : (quad + 1) * UNITS, b, :])
-                col0 = b * T + quad * ROWS
-                quantise_rows(raw_a, UNITS, a_codes, a_scales, [col0, TOKENS + col0])
+            for chunk in range(CHUNKS):
+                quantise_attn(b, chunk)
 
         def project(b, block):
             tok = b * T + block * P
@@ -381,7 +391,7 @@ def tile_multiheadattention820_pa_kernel(tc, v, attn_out, dyn_w, dyn_b, out_proj
                 flip_conv(r - 3)
             if r < n_steps:
                 fetch_window(r)
-            if r < PHASES // UNITS:
-                logits_block(1, r)
-            if r == PHASES // UNITS:
-                read_skewed(1)
+            following = r // ROUNDS_PER_CHUNK + 1
+            if r % ROUNDS_PER_CHUNK == 0 and following < B * CHUNKS:
+                logits_chunk(following // CHUNKS, following % CHUNKS)
+                read_skewed(following // CHUNKS, following % CHUNKS)

@@ -39,6 +39,8 @@ N_GAPS = TAPS * B - 1
 SCRATCH_ROWS = 552
 
 HEADS_PER_PASS = K_PASS // R
+PAIR_HEADS = 9
+F32_HEADS = H - PAIR_HEADS
 
 FLOPS = 2 * TOKENS * E * HK + 2 * TOKENS * (2 * E) * E + 2 * TOKENS * E * TAPS
 
@@ -128,8 +130,7 @@ def tile_multiheadattention820_pa_kernel(tc, v, attn_out, dyn_w, dyn_b, out_proj
                 for gu in range(4):
                     first = n * WORDS + gu * P
                     nc.tensor.transpose(flipped[:, gu * P : (gu + 1) * P], words[:, first : first + P], ident_f32[:])
-                copy_out = nc.vector.tensor_copy if n % UNITS == 2 else nc.scalar.copy
-                copy_out(
+                nc.scalar.copy(
                     out=grouped_words[:, :, n * P : (n + 1) * P, :],
                     in_=flipped[:].rearrange("p (g u r) -> p g r u", g=2, u=2),
                 )
@@ -235,9 +236,7 @@ def tile_multiheadattention820_pa_kernel(tc, v, attn_out, dyn_w, dyn_b, out_proj
             col0 = b * T + chunk * CHUNK
             quantise_rows(raw_a, UNITS, a_codes, a_scales, [col0, TOKENS + col0])
 
-        for b in range(B):
-            for chunk in range(CHUNKS):
-                quantise_attn(b, chunk)
+        quantise_attn(0, 0)
 
         def project(b, block):
             tok = b * T + block * P
@@ -280,17 +279,20 @@ def tile_multiheadattention820_pa_kernel(tc, v, attn_out, dyn_w, dyn_b, out_proj
             t0 = w * WINDOW_STEP
             window_bf16 = win_pool.tile([P, E], BF16)
             nc.sync.dma_start(out=window_bf16[:], in_=v[t0 : t0 + P, b, :])
-            window_f32 = win_pool.tile([P, K_PASS], F32)
+            window_f32 = win_pool.tile([P, F32_HEADS * R], F32)
             nc.gpsimd.tensor_scalar(
-                out=window_f32[:], in0=window_bf16[:, K_PASS:E], scalar1=1.0, scalar2=0.0, op0=ALU.mult, op1=ALU.add
+                out=window_f32[:], in0=window_bf16[:, PAIR_HEADS * R : E], scalar1=1.0, scalar2=0.0,
+                op0=ALU.mult, op1=ALU.add,
             )
             windows[s] = (window_bf16, window_f32)
 
-        def spread(taps, mask):
-            shape = [P, HEADS_PER_PASS, P // TAPS, TAPS]
-            return (
-                taps.rearrange("p (h i) -> p h i", i=TAPS).unsqueeze(2).to_broadcast(shape),
-                mask.rearrange("p (a i) -> p a i", i=TAPS).unsqueeze(1).to_broadcast(shape),
+        def banded(engine, band, taps, mask, heads):
+            shape = [P, heads, P // TAPS, TAPS]
+            engine.tensor_tensor(
+                out=band.rearrange("p (h a i) -> p h a i", h=heads, i=TAPS),
+                in0=taps.rearrange("p (h i) -> p h i", i=TAPS).unsqueeze(2).to_broadcast(shape),
+                in1=mask.rearrange("p (a i) -> p a i", i=TAPS).unsqueeze(1).to_broadcast(shape),
+                op=ALU.mult,
             )
 
         def make_band(s):
@@ -301,25 +303,17 @@ def tile_multiheadattention820_pa_kernel(tc, v, attn_out, dyn_w, dyn_b, out_proj
                 nc.tensor.transpose(
                     by_time[:, half * P : (half + 1) * P], skewed[(b, half)][:, t0 : t0 + P], ident_f32[:]
                 )
-            taps_hi = band_pool.tile([P, P], BF16)
-            nc.scalar.copy(out=taps_hi[:], in_=by_time[:, 0:P])
-            taps_lo = band_pool.tile([P, P], BF16)
-            nc.vector.tensor_tensor(out=taps_lo[:], in0=by_time[:, 0:P], in1=taps_hi[:], op=ALU.subtract)
-            band_hi = band_pool.tile([P, HEADS_PER_PASS * P], BF16)
-            in0, in1 = spread(taps_hi[:], band_mask_bf16[:])
-            nc.vector.tensor_tensor(
-                out=band_hi[:].rearrange("p (h a i) -> p h a i", h=HEADS_PER_PASS, i=TAPS), in0=in0, in1=in1, op=ALU.mult
-            )
-            band_lo = band_pool.tile([P, HEADS_PER_PASS * P], BF16)
-            in0, in1 = spread(taps_lo[:], band_mask_bf16[:])
-            nc.gpsimd.tensor_tensor(
-                out=band_lo[:].rearrange("p (h a i) -> p h a i", h=HEADS_PER_PASS, i=TAPS), in0=in0, in1=in1, op=ALU.mult
-            )
-            band_f32 = band_pool.tile([P, HEADS_PER_PASS * P], F32)
-            in0, in1 = spread(by_time[:, P : 2 * P], band_mask[:])
-            nc.vector.tensor_tensor(
-                out=band_f32[:].rearrange("p (h a i) -> p h a i", h=HEADS_PER_PASS, i=TAPS), in0=in0, in1=in1, op=ALU.mult
-            )
+            pair_cols = PAIR_HEADS * TAPS
+            taps_hi = band_pool.tile([P, pair_cols], BF16)
+            nc.scalar.copy(out=taps_hi[:], in_=by_time[:, 0:pair_cols])
+            taps_lo = band_pool.tile([P, pair_cols], BF16)
+            nc.vector.tensor_tensor(out=taps_lo[:], in0=by_time[:, 0:pair_cols], in1=taps_hi[:], op=ALU.subtract)
+            band_hi = band_pool.tile([P, PAIR_HEADS * P], BF16)
+            banded(nc.vector, band_hi[:], taps_hi[:], band_mask_bf16[:], PAIR_HEADS)
+            band_lo = band_pool.tile([P, PAIR_HEADS * P], BF16)
+            banded(nc.gpsimd, band_lo[:], taps_lo[:], band_mask_bf16[:], PAIR_HEADS)
+            band_f32 = band_pool.tile([P, F32_HEADS * P], F32)
+            banded(nc.vector, band_f32[:], by_time[:, pair_cols:HK], band_mask[:], F32_HEADS)
             bands[s] = (band_hi, band_lo, band_f32)
 
         def convolve(s):
@@ -328,16 +322,19 @@ def tile_multiheadattention820_pa_kernel(tc, v, attn_out, dyn_w, dyn_b, out_proj
             conv_bf16 = conv_pool.tile([P, E], BF16)
             for g in range(2):
                 conv_f32 = conv_psum.tile([P, K_PASS], F32, tag="conv")
-                for h in range(HEADS_PER_PASS):
-                    sums = conv_f32[:, h * R : (h + 1) * R]
-                    one = slice(h * P, (h + 1) * P)
-                    if g == 0:
+                for hl in range(HEADS_PER_PASS):
+                    h = g * HEADS_PER_PASS + hl
+                    sums = conv_f32[:, hl * R : (hl + 1) * R]
+                    if h < PAIR_HEADS:
                         moving = window_bf16[:, h * R : (h + 1) * R]
-                        nc.tensor.matmul(out=sums, lhsT=band_hi[:, one], rhs=moving, start=True, stop=False)
-                        nc.tensor.matmul(out=sums, lhsT=band_lo[:, one], rhs=moving, start=False, stop=True)
+                        nc.tensor.matmul(out=sums, lhsT=band_hi[:, h * P : (h + 1) * P], rhs=moving, start=True, stop=False)
+                        nc.tensor.matmul(out=sums, lhsT=band_lo[:, h * P : (h + 1) * P], rhs=moving, start=False, stop=True)
                     else:
-                        moving = window_f32[:, h * R : (h + 1) * R]
-                        nc.tensor.matmul(out=sums, lhsT=band_f32[:, one], rhs=moving, start=True, stop=True)
+                        f = h - PAIR_HEADS
+                        nc.tensor.matmul(
+                            out=sums, lhsT=band_f32[:, f * P : (f + 1) * P], rhs=window_f32[:, f * R : (f + 1) * R],
+                            start=True, stop=True,
+                        )
                 nc.scalar.copy(
                     out=conv_bf16[:, g * K_PASS : (g + 1) * K_PASS].rearrange("x (u e q) -> x u e q", u=2, e=2),
                     in_=conv_f32[:].rearrange("x (u q e) -> x u e q", u=2, e=2),
@@ -395,3 +392,4 @@ def tile_multiheadattention820_pa_kernel(tc, v, attn_out, dyn_w, dyn_b, out_proj
             if r % ROUNDS_PER_CHUNK == 0 and following < B * CHUNKS:
                 logits_chunk(following // CHUNKS, following % CHUNKS)
                 read_skewed(following // CHUNKS, following % CHUNKS)
+                quantise_attn(following // CHUNKS, following % CHUNKS)

@@ -311,7 +311,7 @@ def tile_multiheadattention820_pa_kernel(tc, v, attn_out, dyn_w, dyn_b, out_proj
             band_hi = band_pool.tile([P, PAIR_HEADS * P], BF16)
             banded(nc.vector, band_hi[:], taps_hi[:], band_mask_bf16[:], PAIR_HEADS)
             band_lo = band_pool.tile([P, PAIR_HEADS * P], BF16)
-            banded(nc.gpsimd, band_lo[:], taps_lo[:], band_mask_bf16[:], PAIR_HEADS)
+            banded(nc.vector, band_lo[:], taps_lo[:], band_mask_bf16[:], PAIR_HEADS)
             band_f32 = band_pool.tile([P, F32_HEADS * P], F32)
             banded(nc.vector, band_f32[:], by_time[:, pair_cols:HK], band_mask[:], F32_HEADS)
             bands[s] = (band_hi, band_lo, band_f32)

@@ -28,19 +28,35 @@ TOKENS = T * B
 
 WINDOW_STEP = P - TAPS
 N_WINDOWS = (T - P) // WINDOW_STEP + 1
-CHUNK = UNITS * P
-CHUNKS = T // CHUNK
-ROUNDS_PER_CHUNK = 4
+SWAP = PAD_L
+MIDDLE_RUNS = WINDOW_STEP // TAPS
 
-PART = T + TAPS
-ROW_PITCH = B * PART
-HEAD_PITCH = TAPS * ROW_PITCH - TAPS
-N_GAPS = TAPS * B - 1
-SCRATCH_ROWS = 552
+RUNS = P // TAPS
+CHUNKS = [(0, 0, 2), (0, 256, 2), (0, 512, 4), (1, 0, 4), (1, 512, 4)]
+
+LAG = TAPS - 1 - PAD_L
+EDGE_ROW = 2 * TAPS
+
+
+def region_words(row):
+    return H * (TAPS * row + TAPS)
+
+
+REGION_WORDS = [region_words(blocks * P) for b, t0, blocks in CHUNKS]
+EDGE_WORDS = region_words(EDGE_ROW)
+REGION_START = [sum(REGION_WORDS[:c]) + c * EDGE_WORDS for c in range(len(CHUNKS))]
+EDGE_START = [REGION_START[c] + REGION_WORDS[c] for c in range(len(CHUNKS))]
+SCRATCH_WORDS = EDGE_START[-1] + EDGE_WORDS + region_words(UNITS * P) // H
 
 HEADS_PER_PASS = K_PASS // R
-PAIR_HEADS = 9
-F32_HEADS = H - PAIR_HEADS
+PAIR_HEADS = HEADS_PER_PASS
+MAX_EXTRA = 2
+EXTRAS = [MAX_EXTRA - w % 2 for w in range(N_WINDOWS)]
+LIMIT_FLOPS = (2 * TOKENS * E * HK + 2 * TOKENS * (2 * E) * E) // 10
+assert B * sum(H + PAIR_HEADS + e for e in EXTRAS) * 2 * P * P * R <= LIMIT_FLOPS
+F32_HEADS = H - PAIR_HEADS - min(EXTRAS)
+WINDOWS_AHEAD = 2
+BAND_SETS = 3
 
 FLOPS = 2 * TOKENS * E * HK + 2 * TOKENS * (2 * E) * E + 2 * TOKENS * E * TAPS
 
@@ -50,22 +66,113 @@ def tile_multiheadattention820_pa_kernel(tc, v, attn_out, dyn_w, dyn_b, out_proj
     with ExitStack() as ctx:
         consts = ctx.enter_context(tc.tile_pool(name="consts", bufs=1))
         keep = ctx.enter_context(tc.tile_pool(name="keep", bufs=1))
-        raw_pool = ctx.enter_context(tc.tile_pool(name="raw", bufs=3))
+        raw_pool = ctx.enter_context(tc.tile_pool(name="raw", bufs=5))
         stage = ctx.enter_context(tc.tile_pool(name="stage", bufs=2))
         vq_pool = ctx.enter_context(tc.tile_pool(name="vq", bufs=2))
-        soft = ctx.enter_context(tc.tile_pool(name="soft", bufs=3))
-        band_pool = ctx.enter_context(tc.tile_pool(name="band", bufs=3))
-        win_pool = ctx.enter_context(tc.tile_pool(name="win", bufs=3))
+        soft = ctx.enter_context(tc.tile_pool(name="soft", bufs=2))
+        skew_pool = ctx.enter_context(tc.tile_pool(name="skew", bufs=2))
+        win_pool = ctx.enter_context(tc.tile_pool(name="win", bufs=4))
+        wide_pool = ctx.enter_context(tc.tile_pool(name="wide", bufs=3))
         conv_pool = ctx.enter_context(tc.tile_pool(name="conv", bufs=3))
+        conv_q_pool = ctx.enter_context(tc.tile_pool(name="convq", bufs=2))
         out_pool = ctx.enter_context(tc.tile_pool(name="outp", bufs=3))
         flip_psum = ctx.enter_context(tc.psum_pool(name="flip", bufs=3))
         conv_psum = ctx.enter_context(tc.psum_pool(name="convp", bufs=3))
         acc_psum = ctx.enter_context(tc.psum_pool(name="acc", bufs=2))
 
+        attn_rows = attn_out.rearrange("(n p) b c -> p n b c", p=P)
+        dyn_rows = dyn_w.rearrange("(n p) c -> p n c", p=P)
+        w_rows = out_proj_w.rearrange("(n p) c -> p n c", p=P)
+        out_rows = out.rearrange("(n p) b e -> p n b e", p=P)
+        scratch = out.rearrange("t b e -> (t b e)")[TOKENS * E - SCRATCH_WORDS : TOKENS * E]
+
+        def load_chunk(c):
+            b, t0, blocks = CHUNKS[c]
+            return load_rows(v[t0 : t0 + blocks * P, b, :].rearrange("(p n) e -> p n e", n=blocks))
+
+        def load_rows(view):
+            raw = raw_pool.tile([P, UNITS * E], BF16, name="raw")
+            blocks = view.shape[1]
+            nc.sync.dma_start(out=raw[:, 0 : blocks * E].rearrange("p (n c) -> p n c", c=E), in_=view)
+            return raw
+
+        def load_w(nh, part):
+            return load_rows(w_rows[:, nh * UNITS : (nh + 1) * UNITS, part * E : (part + 1) * E])
+
+        def load_attn(quarter):
+            b, first = quarter // 2, (quarter % 2) * UNITS
+            return load_rows(attn_rows[:, first : first + UNITS, b, :])
+
+        steps = []
+        for b in range(B):
+            for w in range(N_WINDOWS):
+                steps.append((b, w))
+        windows = {}
+
+        def fetch_window(s):
+            b, w = steps[s]
+            t0 = w * WINDOW_STEP
+            window_bf16 = win_pool.tile([P, E], BF16)
+            nc.sync.dma_start(out=window_bf16[:], in_=v[t0 : t0 + P, b, :])
+            windows[s] = window_bf16
+
+        raw_v0 = load_chunk(0)
+        raw_d = load_rows(dyn_rows)
+        dyn_b_bf16 = consts.tile([P, HK], BF16)
+        nc.sync.dma_start(out=dyn_b_bf16[:], in_=dyn_b.partition_broadcast(P))
+        raw_v1 = load_chunk(1)
+        raw_v2 = load_chunk(2)
+        for s in range(WINDOWS_AHEAD):
+            fetch_window(s)
+        raw_w = {}
+        for nh in range(E // N_TILE):
+            for part in range(2):
+                raw_w[(nh, part)] = load_w(nh, part)
+        raw_a0 = load_attn(0)
+
         ident_f32 = consts.tile([P, P], F32)
         make_identity(nc, ident_f32[:])
-        ident_bf16 = consts.tile([P, P], BF16)
-        make_identity(nc, ident_bf16[:])
+
+        permuted = {}
+        for blocks in sorted({chunk[2] for chunk in CHUNKS}):
+            perm = consts.tile([P, P], F32, name="perm%d" % blocks)
+            steps_of_run = TAPS // blocks
+            for m in range(steps_of_run):
+                nc.vector.tensor_copy(
+                    out=perm[:].rearrange("p (j m q) -> p j m q", j=blocks, q=RUNS)[:, :, m, :],
+                    in_=ident_f32[:].rearrange("p (q j m) -> p j m q", q=RUNS, j=blocks)[:, :, steps_of_run - 1 - m, :],
+                )
+            permuted[blocks] = perm
+
+        zeros = consts.tile([H, TAPS], F32)
+        nc.vector.memset(zeros[:], 0.0)
+        for (b, t0, blocks), start in zip(CHUNKS, REGION_START):
+            pitch = region_words(blocks * P) // H
+            ends = []
+            if t0 == 0:
+                ends.append(start)
+            if t0 + blocks * P == T:
+                ends.append(start + pitch)
+            for first in ends:
+                nc.sync.dma_start(
+                    out=scratch[first : first + H * pitch].rearrange("(h z) -> h z", z=pitch)[:, 0:TAPS], in_=zeros[:]
+                )
+
+        warm = consts.tile([P, 1], F32)
+        nc.vector.memset(warm[:], 0.0)
+        nc.scalar.activation(out=warm[:], in_=warm[:], func=ACT.Exp)
+
+        dyn_b_f32 = consts.tile([P, HK], F32)
+        nc.vector.tensor_copy(out=dyn_b_f32[:], in_=dyn_b_bf16[:])
+
+        reversed_f32 = consts.tile([P, P], F32)
+        by_tap = reversed_f32[:].rearrange("p (h i) -> p h i", i=TAPS)
+        for i in range(TAPS):
+            nc.gpsimd.tensor_copy(
+                out=by_tap[:, :, i : i + 1], in_=ident_f32[:].rearrange("p (h i) -> p h i", i=TAPS)[:, :, TAPS - 1 - i : TAPS - i]
+            )
+        reversed_bf16 = consts.tile([P, P], BF16)
+        nc.vector.tensor_copy(out=reversed_bf16[:], in_=reversed_f32[:])
 
         band_mask = consts.tile([P, P], F32)
         nc.gpsimd.memset(band_mask[:], 1.0)
@@ -78,62 +185,43 @@ def tile_multiheadattention820_pa_kernel(tc, v, attn_out, dyn_w, dyn_b, out_proj
             base=TAPS - 1 - PAD_L, pattern=[[1, P]], channel_multiplier=-1,
         )
 
-        band_mask_bf16 = consts.tile([P, P], BF16)
-        nc.vector.tensor_copy(out=band_mask_bf16[:], in_=band_mask[:])
-
-        dyn_b_bf16 = consts.tile([P, HK], BF16)
-        nc.gpsimd.dma_start(out=dyn_b_bf16[:], in_=dyn_b.partition_broadcast(P))
-        dyn_b_f32 = consts.tile([P, HK], F32)
-        nc.vector.tensor_copy(out=dyn_b_f32[:], in_=dyn_b_bf16[:])
-        out_b_bf16 = consts.tile([P, E], BF16)
-        nc.gpsimd.dma_start(out=out_b_bf16[:], in_=out_proj_b.partition_broadcast(P))
-        out_b_f32 = consts.tile([P, E], F32)
-        nc.vector.tensor_copy(out=out_b_f32[:], in_=out_b_bf16[:])
-
-        v_chunks = v.rearrange("(c p j) b e -> p c j b e", c=CHUNKS, j=UNITS)
-        attn_rows = attn_out.rearrange("(n p) b c -> p n b c", p=P)
-        dyn_rows = dyn_w.rearrange("(n p) c -> p n c", p=P)
-        w_rows = out_proj_w.rearrange("(n p) c -> p n c", p=P)
-        out_rows = out.rearrange("(n p) b e -> p n b e", p=P)
-        scratch = out.rearrange("t b e -> (t b e)")[(TOKENS - SCRATCH_ROWS) * E : TOKENS * E]
-
-        zeros = consts.tile([H, N_GAPS * TAPS], F32)
-        nc.vector.memset(zeros[:], 0.0)
-        gaps = (
-            scratch[0 : H * HEAD_PITCH]
-            .rearrange("(h z) -> h z", z=HEAD_PITCH)[:, 0 : N_GAPS * PART]
-            .rearrange("h (m y) -> h m y", y=PART)[:, :, T:PART]
-        )
-        nc.sync.dma_start(out=gaps, in_=zeros[:].rearrange("h (m y) -> h m y", y=TAPS))
+        swapped_mask = consts.tile([P, P], F32)
+        swapped_ident = consts.tile([P, P], F32)
+        for swapped, source in ((swapped_mask, band_mask), (swapped_ident, ident_f32)):
+            nc.vector.tensor_copy(out=swapped[:], in_=source[:])
+            nc.vector.tensor_copy(out=swapped[:, 0:SWAP], in_=source[:, WINDOW_STEP : WINDOW_STEP + SWAP])
+            nc.vector.tensor_copy(out=swapped[:, WINDOW_STEP : WINDOW_STEP + SWAP], in_=source[:, 0:SWAP])
+        swapped_mask_bf16 = consts.tile([P, P], BF16)
+        nc.vector.tensor_copy(out=swapped_mask_bf16[:], in_=swapped_mask[:])
 
         d_codes = keep.tile([P, 2 * HK], U32, align_bytes=64)
         d_scales = keep.tile([P, 2 * HK], U8, align_bytes=64)
         w_codes = keep.tile([P, 4 * E], U32, align_bytes=64)
         w_scales = keep.tile([P, 4 * E], U8, align_bytes=64)
-        a_codes = keep.tile([P, 2 * TOKENS], U32, align_bytes=64)
-        a_scales = keep.tile([P, 2 * TOKENS], U8, align_bytes=64)
-        c_codes = keep.tile([P, 2 * TOKENS], U32, align_bytes=64)
-        c_scales = keep.tile([P, 2 * TOKENS], U8, align_bytes=64)
+        attn_parts = {}
+        conv_parts = {}
 
-        def load_rows(view):
-            raw = raw_pool.tile([P, UNITS * E], BF16)
-            blocks = view.shape[1]
-            nc.scalar.dma_start(out=raw[:, 0 : blocks * E].rearrange("p (n c) -> p n c", c=E), in_=view)
-            return raw
-
-        def quantise_rows(raw, blocks, codes, scales, pass_cols):
+        def quantise_rows(raw, blocks, codes, scales, pass_cols, of_chunk=False):
             words = raw[:].bitcast(F32)
             grouped = stage.tile([P, 2 * ROWS * PACK], BF16, align_bytes=64)
             grouped_words = grouped[:].bitcast(F32).rearrange("p (g r u) -> p g r u", g=2, u=2)
             for n in range(blocks):
                 flipped = flip_psum.tile([P, 4 * P], F32, tag="flip")
+                order = permuted[blocks] if of_chunk else ident_f32
                 for gu in range(4):
                     first = n * WORDS + gu * P
-                    nc.tensor.transpose(flipped[:, gu * P : (gu + 1) * P], words[:, first : first + P], ident_f32[:])
-                nc.scalar.copy(
-                    out=grouped_words[:, :, n * P : (n + 1) * P, :],
-                    in_=flipped[:].rearrange("p (g u r) -> p g r u", g=2, u=2),
-                )
+                    nc.tensor.transpose(flipped[:, gu * P : (gu + 1) * P], words[:, first : first + P], order[:])
+                if of_chunk:
+                    to = grouped_words[:, :, 0 : blocks * P, :].rearrange("p g (m n q) u -> p n g m q u", m=TAPS, n=blocks)
+                    nc.scalar.copy(
+                        out=to[:, blocks - 1 - n],
+                        in_=flipped[:].rearrange("p (g u m q) -> p g m q u", g=2, u=2, m=TAPS),
+                    )
+                else:
+                    nc.scalar.copy(
+                        out=grouped_words[:, :, n * P : (n + 1) * P, :],
+                        in_=flipped[:].rearrange("p (g u r) -> p g r u", g=2, u=2),
+                    )
             rows = blocks * P
             for g in range(2):
                 cols = slice(pass_cols[g], pass_cols[g] + rows)
@@ -143,7 +231,7 @@ def tile_multiheadattention820_pa_kernel(tc, v, attn_out, dyn_w, dyn_b, out_proj
                     in_=grouped[:, g * ROWS * PACK : g * ROWS * PACK + rows * PACK],
                 )
 
-        def softmax_over_taps(logits):
+        def softmax_over_taps(logits, final):
             groups = 2 * H
             weights = soft.tile([P, 2 * HK], F32)
             by_head = weights[:].rearrange("p (m k) -> p m k", k=TAPS)
@@ -164,21 +252,23 @@ def tile_multiheadattention820_pa_kernel(tc, v, attn_out, dyn_w, dyn_b, out_proj
             inverse = soft.tile([P, groups], F32)
             nc.vector.reciprocal(out=inverse[:], in_=total[:])
             nc.vector.tensor_tensor(
-                out=by_head, in0=by_head, in1=inverse[:].unsqueeze(2).to_broadcast([P, groups, TAPS]), op=ALU.mult
+                out=final,
+                in0=weights[:].rearrange("p (n h k) -> p h n k", n=2, k=TAPS),
+                in1=inverse[:].rearrange("p (n h) -> p h n", n=2).unsqueeze(3).to_broadcast([P, H, 2, TAPS]),
+                op=ALU.mult,
             )
-            return weights
 
-        raw_d = load_rows(dyn_rows)
         quantise_rows(raw_d, 2, d_codes, d_scales, [0, HK])
 
-        skewed = {}
-
-        def logits_chunk(b, chunk):
-            raw_v = load_rows(v_chunks[:, chunk, :, b, :])
+        def logits_chunk(c, raw_v):
+            b, t0, blocks = CHUNKS[c]
             v_codes = vq_pool.tile([P, 2 * ROWS], U32, align_bytes=64)
             v_scales = vq_pool.tile([P, 2 * ROWS], U8, align_bytes=64)
-            quantise_rows(raw_v, UNITS, v_codes, v_scales, [0, ROWS])
-            for pair in range(UNITS // 2):
+            quantise_rows(raw_v, blocks, v_codes, v_scales, [0, ROWS], of_chunk=True)
+            run = blocks * TAPS
+            runs = soft.tile([P, UNITS * HK], F32)
+            by_block = runs[:, 0 : blocks * HK].rearrange("p (h j k) -> p h j k", h=H, k=TAPS)
+            for pair in range(blocks // 2):
                 logits = acc_psum.tile([P, N_TILE], F32, tag="acc")
                 for n in range(2):
                     for g in range(2):
@@ -192,60 +282,178 @@ def tile_multiheadattention820_pa_kernel(tc, v, attn_out, dyn_w, dyn_b, out_proj
                             start=(g == 0),
                             stop=(g == 1),
                         )
-                weights = softmax_over_taps(logits)
-                for n in range(2):
-                    j = 2 * pair + n
-                    for m in range(TAPS // UNITS):
-                        first = (UNITS * m + j) * ROW_PITCH + b * PART + chunk * CHUNK
-                        rows_of_i = (
-                            scratch[first : first + H * HEAD_PITCH]
-                            .rearrange("(h z) -> h z", z=HEAD_PITCH)[:, 0:CHUNK]
-                            .rearrange("h (a k) -> a h k", k=TAPS)
-                        )
-                        nc.sync.dma_start(
-                            out=rows_of_i,
-                            in_=weights[m : P : TAPS // UNITS, n * HK : (n + 1) * HK].rearrange("a (h k) -> a h k", k=TAPS),
-                        )
-
-        def read_skewed(b, chunk):
-            lo = 0 if chunk == 0 else chunk * CHUNK - PAD_L
-            hi = T if chunk == CHUNKS - 1 else (chunk + 1) * CHUNK - PAD_L
-            for half in range(2):
-                if chunk == 0:
-                    skew = keep.tile([P, T], F32, name="skew%d%d" % (b, half))
-                    skewed[(b, half)] = skew
-                first = half * P * (ROW_PITCH - 1) + b * PART + PAD_L
+                softmax_over_taps(logits, by_block[:, :, 2 * pair : 2 * pair + 2, :])
+            def to_scratch(start, row, parts, first, words):
+                pitch = region_words(row) // H
+                by_head = scratch[start : start + H * pitch].rearrange("(h z) -> h z", z=pitch)[:, TAPS:pitch]
+                taps = runs[parts, 0 : blocks * HK].rearrange("p (h y) -> p h y", h=H)[:, :, words]
+                each = TAPS * row // taps.shape[0]
                 nc.sync.dma_start(
-                    out=skewed[(b, half)][:, lo:hi],
-                    in_=scratch[first : first + P * (ROW_PITCH - 1)].rearrange("(p y) -> p y", y=ROW_PITCH - 1)[:, lo:hi],
+                    out=by_head.rearrange("h (p y) -> p h y", y=each)[:, :, first : first + taps.shape[2]], in_=taps
                 )
 
-        logits_chunk(0, 0)
-        read_skewed(0, 0)
+            to_scratch(REGION_START[c], blocks * P, slice(0, P), 0, slice(0, run))
+            if t0 > 0:
+                to_scratch(EDGE_START[c - 1], EDGE_ROW, slice(0, P, RUNS), TAPS, slice(0, TAPS))
+            if t0 + blocks * P < T:
+                to_scratch(EDGE_START[c], EDGE_ROW, slice(RUNS - 1, P, RUNS), 0, slice(run - TAPS, run))
 
-        for nh in range(E // N_TILE):
-            for part in range(2):
-                raw_w = load_rows(w_rows[:, nh * UNITS : (nh + 1) * UNITS, part * E : (part + 1) * E])
-                quantise_rows(
-                    raw_w, UNITS, w_codes, w_scales,
-                    [(2 * part) * E + nh * N_TILE, (2 * part + 1) * E + nh * N_TILE],
+        skewed = []
+        for b in range(B):
+            taps_hi = keep.tile([P, T], BF16, name="hi%d" % b)
+            taps_lo = keep.tile([P, T], BF16, name="lo%d" % b)
+            taps_f32 = keep.tile([P, T], F32, name="taps_f32%d" % b)
+            skewed.append((taps_hi, taps_lo, taps_f32))
+
+        def read_skewed(c):
+            b, t0, blocks = CHUNKS[c]
+            end = t0 + blocks * P
+            pieces = [(REGION_START[c], blocks * P, t0, 0 if t0 == 0 else t0 + PAD_L, T if end == T else end - PAD_L)]
+            if t0 > 0:
+                pieces = [(EDGE_START[c - 1], EDGE_ROW, t0 - TAPS, t0 - PAD_L, t0 + PAD_L)] + pieces
+            taps_hi, taps_lo, taps_f32 = skewed[b]
+            skew = skew_pool.tile([P, ROWS + TAPS], F32)
+            first_col = pieces[0][3]
+            last_col = pieces[-1][4]
+            for start, row, origin, lo, hi in pieces:
+                for half in range(2):
+                    into = skew[:, lo - first_col : hi - first_col] if half == 0 else taps_f32[:, lo:hi]
+                    first = start + half * P * (row + 1) + TAPS - LAG
+                    nc.sync.dma_start(
+                        out=into,
+                        in_=scratch[first : first + P * (row + 1)].rearrange("(p y) -> p y", y=row + 1)[:, lo - origin : hi - origin],
+                    )
+            first_heads = skew[:, 0 : last_col - first_col]
+            cols = slice(first_col, last_col)
+            nc.scalar.copy(out=taps_hi[:, cols], in_=first_heads)
+            nc.vector.tensor_tensor(out=taps_lo[:, cols], in0=first_heads, in1=taps_hi[:, cols], op=ALU.subtract)
+
+        wide_windows = {}
+        bands = []
+        for n in range(BAND_SETS):
+            band_pair = keep.tile([P, 2 * PAIR_HEADS * P], BF16, name="band_pair%d" % n)
+            band_extra = keep.tile([P, 2 * MAX_EXTRA * P], BF16, name="band_extra%d" % n)
+            band_f32 = keep.tile([P, F32_HEADS * P], F32, name="band_f32%d" % n)
+            for band in (band_pair, band_extra, band_f32):
+                nc.gpsimd.memset(band[:].rearrange("p (m x) -> p m x", x=P)[:, :, WINDOW_STEP:P], 0.0)
+            bands.append((band_pair, band_extra, band_f32))
+        taps_x = {}
+        conv_tiles = {}
+        finished = {}
+        grouped_conv = keep.tile([P, 2 * T * PACK], BF16, align_bytes=64)
+        grouped_conv_words = grouped_conv[:].bitcast(F32).rearrange("p (g n u) -> p g n u", g=2, u=2)
+
+        def widen_window(s):
+            window_f32 = wide_pool.tile([P, F32_HEADS * R], F32)
+            nc.gpsimd.tensor_scalar(
+                out=window_f32[:], in0=windows[s][:, E - F32_HEADS * R : E], scalar1=1.0, scalar2=0.0,
+                op0=ALU.mult, op1=ALU.add,
+            )
+            wide_windows[s] = window_f32
+
+        def banded(band, taps, mask, matrices, runs):
+            shape = [P, matrices, runs, TAPS]
+            nc.vector.tensor_tensor(
+                out=band.rearrange("p (m a i) -> p m a i", m=matrices, i=TAPS)[:, :, 0:runs, :],
+                in0=taps.rearrange("p (m i) -> p m i", i=TAPS).unsqueeze(2).to_broadcast(shape),
+                in1=mask.rearrange("p (a i) -> p a i", i=TAPS)[:, 0:runs, :].unsqueeze(1).to_broadcast(shape),
+                op=ALU.mult,
+            )
+
+        def make_band(s):
+            b, w = steps[s]
+            t0 = w * WINDOW_STEP
+            taps_hi, taps_lo, taps_f32 = skewed[b]
+            by_time = flip_psum.tile([P, 2 * P], F32, tag="flip")
+            by_time_bf16 = by_time[:, 0:P].bitcast(BF16)
+            nc.tensor.transpose(by_time_bf16[:, 0:P], taps_hi[:, t0 : t0 + P], reversed_bf16[:])
+            nc.tensor.transpose(by_time_bf16[:, P : 2 * P], taps_lo[:, t0 : t0 + P], reversed_bf16[:])
+            nc.tensor.transpose(by_time[:, P : 2 * P], taps_f32[:, t0 : t0 + P], reversed_f32[:])
+            band_pair, band_extra, band_f32 = bands[s % BAND_SETS]
+            runs = MIDDLE_RUNS if 0 < w < N_WINDOWS - 1 else P // TAPS
+            extra = EXTRAS[w]
+            wide = extra * TAPS
+            in_f32 = by_time[:, P + wide : 2 * P]
+            taps_extra = wide_pool.tile([P, 2 * MAX_EXTRA * TAPS], BF16)
+            nc.scalar.copy(out=taps_extra[:, 0:wide], in_=by_time[:, P : P + wide])
+            banded(band_pair[:], by_time_bf16, swapped_mask_bf16[:], 2 * PAIR_HEADS, runs)
+            nc.vector.tensor_tensor(
+                out=taps_extra[:, wide : 2 * wide], in0=by_time[:, P : P + wide], in1=taps_extra[:, 0:wide], op=ALU.subtract
+            )
+            banded(band_f32[:, 0 : (PAIR_HEADS - extra) * P], in_f32, swapped_mask[:], PAIR_HEADS - extra, runs)
+            banded(band_extra[:, 0 : 2 * extra * P], taps_extra[:, 0 : 2 * wide], swapped_mask_bf16[:], 2 * extra, runs)
+
+        def convolve(s):
+            window_bf16, window_f32 = windows[s], wide_windows[s]
+            band_pair, band_extra, band_f32 = bands[s % BAND_SETS]
+            extra = EXTRAS[steps[s][1]]
+            conv_bf16 = conv_pool.tile([P, E], BF16)
+            for g in range(2):
+                conv_f32 = conv_psum.tile([P, K_PASS], F32, tag="conv")
+                for hl in range(HEADS_PER_PASS):
+                    sums = conv_f32[:, hl * R : (hl + 1) * R]
+                    h = g * HEADS_PER_PASS + hl
+                    in_pairs = PAIR_HEADS if g == 0 else extra
+                    if hl < in_pairs:
+                        band = band_pair if g == 0 else band_extra
+                        for part in range(2):
+                            m = part * in_pairs + hl
+                            nc.tensor.matmul(
+                                out=sums, lhsT=band[:, m * P : (m + 1) * P], rhs=window_bf16[:, h * R : (h + 1) * R],
+                                start=(part == 0), stop=(part == 1),
+                            )
+                    else:
+                        m = hl - extra
+                        f = h - (H - F32_HEADS)
+                        nc.tensor.matmul(
+                            out=sums, lhsT=band_f32[:, m * P : (m + 1) * P], rhs=window_f32[:, f * R : (f + 1) * R],
+                            start=True, stop=True,
+                        )
+                nc.scalar.copy(out=conv_bf16[:, g * K_PASS : (g + 1) * K_PASS], in_=conv_f32[:])
+            conv_tiles[s] = conv_bf16
+
+        def flip_conv(s):
+            w = steps[s][1]
+            t0 = w * WINDOW_STEP
+            flipped_conv = flip_psum.tile([P, 4 * P], F32, tag="flip")
+            conv_words = conv_tiles[s][:].bitcast(F32)
+            for gu in range(4):
+                nc.tensor.transpose(
+                    flipped_conv[:, gu * P : (gu + 1) * P], conv_words[:, gu * P : (gu + 1) * P], swapped_ident[:]
                 )
+            lo = 0 if w == 0 else PAD_L
+            hi = P if w == N_WINDOWS - 1 else P - PAD_L
+            nc.scalar.copy(
+                out=grouped_conv_words[:, :, t0 + lo : t0 + hi, :],
+                in_=flipped_conv[:].rearrange("p (g u x) -> p g x u", g=2, u=2)[:, :, lo:hi, :],
+            )
+            first_block = 0 if w == 0 else (t0 - WINDOW_STEP + P - PAD_L) // P
+            finished[s] = list(range(first_block, (t0 + hi) // P))
 
-        def quantise_attn(b, chunk):
-            raw_a = load_rows(attn_rows[:, chunk * UNITS : (chunk + 1) * UNITS, b, :])
-            col0 = b * T + chunk * CHUNK
-            quantise_rows(raw_a, UNITS, a_codes, a_scales, [col0, TOKENS + col0])
-
-        quantise_attn(0, 0)
+        def quantise_conv(s):
+            b = steps[s][0]
+            for block in finished[s]:
+                quarter, tok = divmod(b * T + block * P, ROWS)
+                if tok == 0:
+                    c_codes = conv_q_pool.tile([P, 2 * ROWS], U32, align_bytes=64)
+                    c_scales = conv_q_pool.tile([P, 2 * ROWS], U8, align_bytes=64)
+                    conv_parts[quarter] = (c_codes, c_scales)
+                c_codes, c_scales = conv_parts[quarter]
+                for g in range(2):
+                    first = (g * T + block * P) * PACK
+                    cols = slice(g * ROWS + tok, g * ROWS + tok + P)
+                    nc.vector.quantize_mx(
+                        out=c_codes[:, cols].bitcast(FP8X4), scales=c_scales[:, cols], in_=grouped_conv[:, first : first + P * PACK]
+                    )
 
         def project(b, block):
-            tok = b * T + block * P
+            quarter, tok = divmod(b * T + block * P, ROWS)
             result = out_pool.tile([P, E], F32)
             for nh in range(E // N_TILE):
                 acc = acc_psum.tile([P, N_TILE], F32, tag="acc")
                 for c in range(4):
-                    codes, scales = (a_codes, a_scales) if c < 2 else (c_codes, c_scales)
-                    cols = slice((c % 2) * TOKENS + tok, (c % 2) * TOKENS + tok + P)
+                    codes, scales = attn_parts[quarter] if c < 2 else conv_parts[quarter]
+                    cols = slice((c % 2) * ROWS + tok, (c % 2) * ROWS + tok + P)
                     outs = slice(c * E + nh * N_TILE, c * E + (nh + 1) * N_TILE)
                     nc.tensor.matmul_mx(
                         out=acc[:],
@@ -264,117 +472,49 @@ def tile_multiheadattention820_pa_kernel(tc, v, attn_out, dyn_w, dyn_b, out_proj
                 )
             nc.sync.dma_start(out=out_rows[:, block, b, :], in_=result[:])
 
-        steps = []
-        for b in range(B):
-            for w in range(N_WINDOWS):
-                steps.append((b, w))
-        windows = {}
-        bands = {}
-        conv_tiles = {}
-        conv_groups = {}
-        finished = {}
-
-        def fetch_window(s):
-            b, w = steps[s]
-            t0 = w * WINDOW_STEP
-            window_bf16 = win_pool.tile([P, E], BF16)
-            nc.sync.dma_start(out=window_bf16[:], in_=v[t0 : t0 + P, b, :])
-            window_f32 = win_pool.tile([P, F32_HEADS * R], F32)
-            nc.gpsimd.tensor_scalar(
-                out=window_f32[:], in0=window_bf16[:, PAIR_HEADS * R : E], scalar1=1.0, scalar2=0.0,
-                op0=ALU.mult, op1=ALU.add,
-            )
-            windows[s] = (window_bf16, window_f32)
-
-        def banded(engine, band, taps, mask, heads):
-            shape = [P, heads, P // TAPS, TAPS]
-            engine.tensor_tensor(
-                out=band.rearrange("p (h a i) -> p h a i", h=heads, i=TAPS),
-                in0=taps.rearrange("p (h i) -> p h i", i=TAPS).unsqueeze(2).to_broadcast(shape),
-                in1=mask.rearrange("p (a i) -> p a i", i=TAPS).unsqueeze(1).to_broadcast(shape),
-                op=ALU.mult,
+        def quantise_w(nh, part):
+            quantise_rows(
+                raw_w[(nh, part)], UNITS, w_codes, w_scales,
+                [(2 * part) * E + nh * N_TILE, (2 * part + 1) * E + nh * N_TILE],
             )
 
-        def make_band(s):
-            b, w = steps[s]
-            t0 = w * WINDOW_STEP
-            by_time = flip_psum.tile([P, HK], F32, tag="flip")
-            for half in range(2):
-                nc.tensor.transpose(
-                    by_time[:, half * P : (half + 1) * P], skewed[(b, half)][:, t0 : t0 + P], ident_f32[:]
-                )
-            pair_cols = PAIR_HEADS * TAPS
-            taps_hi = band_pool.tile([P, pair_cols], BF16)
-            nc.scalar.copy(out=taps_hi[:], in_=by_time[:, 0:pair_cols])
-            taps_lo = band_pool.tile([P, pair_cols], BF16)
-            nc.vector.tensor_tensor(out=taps_lo[:], in0=by_time[:, 0:pair_cols], in1=taps_hi[:], op=ALU.subtract)
-            band_hi = band_pool.tile([P, PAIR_HEADS * P], BF16)
-            banded(nc.vector, band_hi[:], taps_hi[:], band_mask_bf16[:], PAIR_HEADS)
-            band_lo = band_pool.tile([P, PAIR_HEADS * P], BF16)
-            banded(nc.vector, band_lo[:], taps_lo[:], band_mask_bf16[:], PAIR_HEADS)
-            band_f32 = band_pool.tile([P, F32_HEADS * P], F32)
-            banded(nc.vector, band_f32[:], by_time[:, pair_cols:HK], band_mask[:], F32_HEADS)
-            bands[s] = (band_hi, band_lo, band_f32)
+        def quantise_attn(quarter, raw_a):
+            a_codes = keep.tile([P, 2 * ROWS], U32, align_bytes=64, name="a_codes%d" % quarter)
+            a_scales = keep.tile([P, 2 * ROWS], U8, align_bytes=64, name="a_scales%d" % quarter)
+            attn_parts[quarter] = (a_codes, a_scales)
+            quantise_rows(raw_a, UNITS, a_codes, a_scales, [0, ROWS])
 
-        def convolve(s):
-            window_bf16, window_f32 = windows[s]
-            band_hi, band_lo, band_f32 = bands[s]
-            conv_bf16 = conv_pool.tile([P, E], BF16)
-            for g in range(2):
-                conv_f32 = conv_psum.tile([P, K_PASS], F32, tag="conv")
-                for hl in range(HEADS_PER_PASS):
-                    h = g * HEADS_PER_PASS + hl
-                    sums = conv_f32[:, hl * R : (hl + 1) * R]
-                    if h < PAIR_HEADS:
-                        moving = window_bf16[:, h * R : (h + 1) * R]
-                        nc.tensor.matmul(out=sums, lhsT=band_hi[:, h * P : (h + 1) * P], rhs=moving, start=True, stop=False)
-                        nc.tensor.matmul(out=sums, lhsT=band_lo[:, h * P : (h + 1) * P], rhs=moving, start=False, stop=True)
-                    else:
-                        f = h - PAIR_HEADS
-                        nc.tensor.matmul(
-                            out=sums, lhsT=band_f32[:, f * P : (f + 1) * P], rhs=window_f32[:, f * R : (f + 1) * R],
-                            start=True, stop=True,
-                        )
-                nc.scalar.copy(
-                    out=conv_bf16[:, g * K_PASS : (g + 1) * K_PASS].rearrange("x (u e q) -> x u e q", u=2, e=2),
-                    in_=conv_f32[:].rearrange("x (u q e) -> x u e q", u=2, e=2),
-                )
-            conv_tiles[s] = conv_bf16
+        logits_chunk(0, raw_v0)
+        read_skewed(0)
+        logits_chunk(1, raw_v1)
+        read_skewed(1)
+        out_b_bf16 = consts.tile([P, E], BF16)
+        nc.sync.dma_start(out=out_b_bf16[:], in_=out_proj_b.partition_broadcast(P))
+        out_b_f32 = consts.tile([P, E], F32)
+        nc.vector.tensor_copy(out=out_b_f32[:], in_=out_b_bf16[:])
 
-        def flip_conv(s):
-            b, w = steps[s]
-            t0 = w * WINDOW_STEP
-            if w == 0:
-                grouped_conv = keep.tile([P, 2 * T * PACK], BF16, align_bytes=64)
-                conv_groups[b] = grouped_conv
-            flipped_conv = flip_psum.tile([P, 2 * PACK * P], BF16, tag="flip")
-            for n in range(2 * PACK):
-                nc.tensor.transpose(
-                    flipped_conv[:, n * P : (n + 1) * P], conv_tiles[s][:, n * P : (n + 1) * P], ident_bf16[:]
-                )
-            lo = 0 if w == 0 else PAD_L
-            hi = P if w == N_WINDOWS - 1 else P - PAD_L
-            nc.scalar.copy(
-                out=conv_groups[b][:].rearrange("p (g n t) -> p g n t", g=2, t=PACK)[:, :, t0 + lo : t0 + hi, :],
-                in_=flipped_conv[:].rearrange("p (g t x) -> p g x t", g=2, t=PACK)[:, :, lo:hi, :],
-            )
-            first_block = 0 if w == 0 else (t0 - WINDOW_STEP + P - PAD_L) // P
-            finished[s] = list(range(first_block, (t0 + hi) // P))
+        def chunk_of_logits(c, raw_v):
+            logits_chunk(c, raw_v)
+            read_skewed(c)
 
-        def quantise_conv(s):
-            b = steps[s][0]
-            for block in finished[s]:
-                tok = b * T + block * P
-                for g in range(2):
-                    first = (g * T + block * P) * PACK
-                    nc.vector.quantize_mx(
-                        out=c_codes[:, g * TOKENS + tok : g * TOKENS + tok + P].bitcast(FP8X4),
-                        scales=c_scales[:, g * TOKENS + tok : g * TOKENS + tok + P],
-                        in_=conv_groups[b][:, first : first + P * PACK],
-                    )
+        others = {
+            0: [lambda: quantise_w(0, 0)],
+            1: [lambda: chunk_of_logits(2, raw_v2)],
+            2: [lambda: quantise_w(0, 1), lambda: quantise_w(1, 0)],
+            3: [lambda: quantise_w(1, 1), lambda: quantise_attn(0, raw_a0)],
+            4: [lambda: quantise_attn(1, load_attn(1))],
+            5: [lambda: chunk_of_logits(3, load_chunk(3))],
+            7: [lambda: quantise_attn(2, load_attn(2))],
+            8: [lambda: chunk_of_logits(4, load_chunk(4))],
+            10: [lambda: quantise_attn(3, load_attn(3))],
+        }
 
         n_steps = len(steps)
         for r in range(n_steps + 5):
+            if r < n_steps:
+                widen_window(r)
+            if WINDOWS_AHEAD <= r + 1 < n_steps:
+                fetch_window(r + 1)
             if 1 <= r < n_steps + 1:
                 make_band(r - 1)
             if r >= 5:
@@ -386,10 +526,5 @@ def tile_multiheadattention820_pa_kernel(tc, v, attn_out, dyn_w, dyn_b, out_proj
                 convolve(r - 2)
             if 3 <= r < n_steps + 3:
                 flip_conv(r - 3)
-            if r < n_steps:
-                fetch_window(r)
-            following = r // ROUNDS_PER_CHUNK + 1
-            if r % ROUNDS_PER_CHUNK == 0 and following < B * CHUNKS:
-                logits_chunk(following // CHUNKS, following % CHUNKS)
-                read_skewed(following // CHUNKS, following % CHUNKS)
-                quantise_attn(following // CHUNKS, following % CHUNKS)
+            for task in others.get(r, []):
+                task()

@@ -345,10 +345,7 @@ def tile_multiheadattention820_pa_kernel(tc, v, attn_out, dyn_w, dyn_b, out_proj
 
         def widen_window(s):
             window_f32 = wide_pool.tile([P, F32_HEADS * R], F32)
-            nc.gpsimd.tensor_scalar(
-                out=window_f32[:], in0=windows[s][:, E - F32_HEADS * R : E], scalar1=1.0, scalar2=0.0,
-                op0=ALU.mult, op1=ALU.add,
-            )
+            nc.scalar.copy(out=window_f32[:], in_=windows[s][:, E - F32_HEADS * R : E])
             wide_windows[s] = window_f32
 
         def banded(band, taps, mask, matrices, runs):
@@ -373,14 +370,17 @@ def tile_multiheadattention820_pa_kernel(tc, v, attn_out, dyn_w, dyn_b, out_proj
             runs = MIDDLE_RUNS if 0 < w < N_WINDOWS - 1 else P // TAPS
             extra = EXTRAS[w]
             wide = extra * TAPS
-            in_f32 = by_time[:, P + wide : 2 * P]
+            taps_pair = wide_pool.tile([P, 2 * P], BF16)
+            nc.scalar.copy(out=taps_pair[:], in_=by_time_bf16)
+            taps_rest = wide_pool.tile([P, P], F32)
+            nc.scalar.copy(out=taps_rest[:], in_=by_time[:, P : 2 * P])
             taps_extra = wide_pool.tile([P, 2 * MAX_EXTRA * TAPS], BF16)
-            nc.scalar.copy(out=taps_extra[:, 0:wide], in_=by_time[:, P : P + wide])
-            banded(band_pair[:], by_time_bf16, swapped_mask_bf16[:], 2 * PAIR_HEADS, runs)
+            nc.scalar.copy(out=taps_extra[:, 0:wide], in_=taps_rest[:, 0:wide])
+            banded(band_pair[:], taps_pair[:], swapped_mask_bf16[:], 2 * PAIR_HEADS, runs)
             nc.vector.tensor_tensor(
-                out=taps_extra[:, wide : 2 * wide], in0=by_time[:, P : P + wide], in1=taps_extra[:, 0:wide], op=ALU.subtract
+                out=taps_extra[:, wide : 2 * wide], in0=taps_rest[:, 0:wide], in1=taps_extra[:, 0:wide], op=ALU.subtract
             )
-            banded(band_f32[:, 0 : (PAIR_HEADS - extra) * P], in_f32, swapped_mask[:], PAIR_HEADS - extra, runs)
+            banded(band_f32[:, 0 : (PAIR_HEADS - extra) * P], taps_rest[:, wide:P], swapped_mask[:], PAIR_HEADS - extra, runs)
             banded(band_extra[:, 0 : 2 * extra * P], taps_extra[:, 0 : 2 * wide], swapped_mask_bf16[:], 2 * extra, runs)
 
         def convolve(s):

@@ -76,8 +76,8 @@ def tile_multiheadattention820_pa_kernel(tc, v, attn_out, dyn_w, dyn_b, out_proj
         conv_pool = ctx.enter_context(tc.tile_pool(name="conv", bufs=3))
         conv_q_pool = ctx.enter_context(tc.tile_pool(name="convq", bufs=2))
         out_pool = ctx.enter_context(tc.tile_pool(name="outp", bufs=3))
-        flip_psum = ctx.enter_context(tc.psum_pool(name="flip", bufs=3))
-        conv_psum = ctx.enter_context(tc.psum_pool(name="convp", bufs=3))
+        flip_psum = ctx.enter_context(tc.psum_pool(name="flip", bufs=4))
+        conv_psum = ctx.enter_context(tc.psum_pool(name="convp", bufs=2))
         acc_psum = ctx.enter_context(tc.psum_pool(name="acc", bufs=2))
 
         attn_rows = attn_out.rearrange("(n p) b c -> p n b c", p=P)
@@ -201,27 +201,33 @@ def tile_multiheadattention820_pa_kernel(tc, v, attn_out, dyn_w, dyn_b, out_proj
         attn_parts = {}
         conv_parts = {}
 
-        def quantise_rows(raw, blocks, codes, scales, pass_cols, of_chunk=False):
-            words = raw[:].bitcast(F32)
+        def new_job(raw, blocks, codes, scales, pass_cols, of_chunk=False):
             grouped = stage.tile([P, 2 * ROWS * PACK], BF16, align_bytes=64)
+            return (raw, blocks, codes, scales, pass_cols, of_chunk, grouped)
+
+        def flip_block(job, n):
+            raw, blocks, codes, scales, pass_cols, of_chunk, grouped = job
+            words = raw[:].bitcast(F32)
             grouped_words = grouped[:].bitcast(F32).rearrange("p (g r u) -> p g r u", g=2, u=2)
-            for n in range(blocks):
-                flipped = flip_psum.tile([P, 4 * P], F32, tag="flip")
-                order = permuted[blocks] if of_chunk else ident_f32
-                for gu in range(4):
-                    first = n * WORDS + gu * P
-                    nc.tensor.transpose(flipped[:, gu * P : (gu + 1) * P], words[:, first : first + P], order[:])
-                if of_chunk:
-                    to = grouped_words[:, :, 0 : blocks * P, :].rearrange("p g (m n q) u -> p n g m q u", m=TAPS, n=blocks)
-                    nc.scalar.copy(
-                        out=to[:, blocks - 1 - n],
-                        in_=flipped[:].rearrange("p (g u m q) -> p g m q u", g=2, u=2, m=TAPS),
-                    )
-                else:
-                    nc.scalar.copy(
-                        out=grouped_words[:, :, n * P : (n + 1) * P, :],
-                        in_=flipped[:].rearrange("p (g u r) -> p g r u", g=2, u=2),
-                    )
+            flipped = flip_psum.tile([P, 4 * P], F32, tag="flip")
+            order = permuted[blocks] if of_chunk else ident_f32
+            for gu in range(4):
+                first = n * WORDS + gu * P
+                nc.tensor.transpose(flipped[:, gu * P : (gu + 1) * P], words[:, first : first + P], order[:])
+            if of_chunk:
+                to = grouped_words[:, :, 0 : blocks * P, :].rearrange("p g (m n q) u -> p n g m q u", m=TAPS, n=blocks)
+                nc.scalar.copy(
+                    out=to[:, blocks - 1 - n],
+                    in_=flipped[:].rearrange("p (g u m q) -> p g m q u", g=2, u=2, m=TAPS),
+                )
+            else:
+                nc.scalar.copy(
+                    out=grouped_words[:, :, n * P : (n + 1) * P, :],
+                    in_=flipped[:].rearrange("p (g u r) -> p g r u", g=2, u=2),
+                )
+
+        def quantise_job(job):
+            raw, blocks, codes, scales, pass_cols, of_chunk, grouped = job
             rows = blocks * P
             for g in range(2):
                 cols = slice(pass_cols[g], pass_cols[g] + rows)
@@ -230,6 +236,12 @@ def tile_multiheadattention820_pa_kernel(tc, v, attn_out, dyn_w, dyn_b, out_proj
                     scales=scales[:, cols],
                     in_=grouped[:, g * ROWS * PACK : g * ROWS * PACK + rows * PACK],
                 )
+
+        def flip_blocks(job, first, count):
+            for n in range(first, first + count):
+                flip_block(job, n)
+            if first + count == job[1]:
+                quantise_job(job)
 
         def softmax_over_taps(logits, final):
             groups = 2 * H
@@ -258,13 +270,15 @@ def tile_multiheadattention820_pa_kernel(tc, v, attn_out, dyn_w, dyn_b, out_proj
                 op=ALU.mult,
             )
 
-        quantise_rows(raw_d, 2, d_codes, d_scales, [0, HK])
 
-        def logits_chunk(c, raw_v):
-            b, t0, blocks = CHUNKS[c]
+        def chunk_job(c, raw):
             v_codes = vq_pool.tile([P, 2 * ROWS], U32, align_bytes=64)
             v_scales = vq_pool.tile([P, 2 * ROWS], U8, align_bytes=64)
-            quantise_rows(raw_v, blocks, v_codes, v_scales, [0, ROWS], of_chunk=True)
+            return new_job(raw, CHUNKS[c][2], v_codes, v_scales, [0, ROWS], of_chunk=True)
+
+        def logits_chunk(c, job):
+            b, t0, blocks = CHUNKS[c]
+            v_codes, v_scales = job[2], job[3]
             run = blocks * TAPS
             runs = soft.tile([P, UNITS * HK], F32)
             by_block = runs[:, 0 : blocks * HK].rearrange("p (h j k) -> p h j k", h=H, k=TAPS)
@@ -472,59 +486,91 @@ def tile_multiheadattention820_pa_kernel(tc, v, attn_out, dyn_w, dyn_b, out_proj
                 )
             nc.sync.dma_start(out=out_rows[:, block, b, :], in_=result[:])
 
-        def quantise_w(nh, part):
-            quantise_rows(
-                raw_w[(nh, part)], UNITS, w_codes, w_scales,
-                [(2 * part) * E + nh * N_TILE, (2 * part + 1) * E + nh * N_TILE],
-            )
+        def w_job(nh, part, raw):
+            pass_cols = [(2 * part + g) * E + nh * N_TILE for g in range(2)]
+            return new_job(raw, UNITS, w_codes, w_scales, pass_cols)
 
-        def quantise_attn(quarter, raw_a):
+        def attn_job(quarter, raw_a):
             a_codes = keep.tile([P, 2 * ROWS], U32, align_bytes=64, name="a_codes%d" % quarter)
             a_scales = keep.tile([P, 2 * ROWS], U8, align_bytes=64, name="a_scales%d" % quarter)
             attn_parts[quarter] = (a_codes, a_scales)
-            quantise_rows(raw_a, UNITS, a_codes, a_scales, [0, ROWS])
+            return new_job(raw_a, UNITS, a_codes, a_scales, [0, ROWS])
 
-        logits_chunk(0, raw_v0)
+        ctx.enter_context(tc.manual_schedule(engines={mybir.EngineType.PE}))
+
+        flip_blocks(new_job(raw_d, 2, d_codes, d_scales, [0, HK]), 0, 2)
+        jobs = {}
+        jobs["c0"] = chunk_job(0, raw_v0)
+        flip_blocks(jobs["c0"], 0, 2)
+        jobs["c1"] = chunk_job(1, raw_v1)
+        flip_blocks(jobs["c1"], 0, 2)
+        logits_chunk(0, jobs["c0"])
         read_skewed(0)
-        logits_chunk(1, raw_v1)
+        jobs["c2"] = chunk_job(2, raw_v2)
+        flip_blocks(jobs["c2"], 0, 2)
+        logits_chunk(1, jobs["c1"])
         read_skewed(1)
+        flip_blocks(jobs["c2"], 2, 2)
+        flip_blocks(w_job(0, 0, raw_w[(0, 0)]), 0, UNITS)
+        logits_chunk(2, jobs["c2"])
+        read_skewed(2)
+        flip_blocks(w_job(0, 1, raw_w[(0, 1)]), 0, UNITS)
         out_b_bf16 = consts.tile([P, E], BF16)
         nc.sync.dma_start(out=out_b_bf16[:], in_=out_proj_b.partition_broadcast(P))
         out_b_f32 = consts.tile([P, E], F32)
         nc.vector.tensor_copy(out=out_b_f32[:], in_=out_b_bf16[:])
 
-        def chunk_of_logits(c, raw_v):
-            logits_chunk(c, raw_v)
-            read_skewed(c)
-
-        others = {
-            0: [lambda: quantise_w(0, 0)],
-            1: [lambda: chunk_of_logits(2, raw_v2)],
-            2: [lambda: quantise_w(0, 1), lambda: quantise_w(1, 0)],
-            3: [lambda: quantise_w(1, 1), lambda: quantise_attn(0, raw_a0)],
-            4: [lambda: quantise_attn(1, load_attn(1))],
-            5: [lambda: chunk_of_logits(3, load_chunk(3))],
-            7: [lambda: quantise_attn(2, load_attn(2))],
-            8: [lambda: chunk_of_logits(4, load_chunk(4))],
-            10: [lambda: quantise_attn(3, load_attn(3))],
+        fillers = {
+            0: ("w", (1, 0), 0, 4),
+            1: ("w", (1, 1), 0, 4),
+            2: ("a", 0, 0, 4),
+            3: ("c", 3, 0, 2),
+            4: ("c", 3, 2, 2),
+            5: ("a", 1, 0, 2),
+            6: ("a", 1, 2, 2),
+            7: ("c", 4, 0, 2),
+            8: ("c", 4, 2, 2),
+            9: ("a", 2, 0, 2),
+            10: ("a", 2, 2, 2),
+            11: ("a", 3, 0, 2),
+            12: ("a", 3, 2, 2),
         }
+        raws = {("w", (1, 0)): raw_w[(1, 0)], ("w", (1, 1)): raw_w[(1, 1)], ("a", 0): raw_a0}
+
+        def load_filler(r):
+            kind, number, first, count = fillers.get(r, ("", 0, 1, 0))
+            if first == 0 and (kind, number) not in raws:
+                raws[(kind, number)] = load_chunk(number) if kind == "c" else load_attn(number)
+
+        def flip_filler(r):
+            kind, number, first, count = fillers.get(r, ("", 0, 0, 0))
+            if count > 0:
+                if first == 0:
+                    make = {"w": lambda m, raw: w_job(m[0], m[1], raw), "a": attn_job, "c": chunk_job}[kind]
+                    jobs[(kind, number)] = make(number, raws[(kind, number)])
+                flip_blocks(jobs[(kind, number)], first, count)
+
+        def finish_filler(r):
+            kind, number, first, count = fillers.get(r, ("", 0, 0, 0))
+            if kind == "c" and first + count == UNITS:
+                logits_chunk(number, jobs[(kind, number)])
+                read_skewed(number)
 
         n_steps = len(steps)
-        for r in range(n_steps + 5):
-            if r < n_steps:
-                widen_window(r)
+        for r in range(n_steps + 2):
             if WINDOWS_AHEAD <= r + 1 < n_steps:
                 fetch_window(r + 1)
+            load_filler(r + 2)
+            if r < n_steps:
+                make_band(r)
+                widen_window(r)
+            if r >= 2:
+                flip_conv(r - 2)
+                quantise_conv(r - 2)
+            flip_filler(r)
             if 1 <= r < n_steps + 1:
-                make_band(r - 1)
-            if r >= 5:
-                for block in finished[r - 5]:
-                    project(steps[r - 5][0], block)
-            if 4 <= r < n_steps + 4:
-                quantise_conv(r - 4)
-            if 2 <= r < n_steps + 2:
-                convolve(r - 2)
-            if 3 <= r < n_steps + 3:
-                flip_conv(r - 3)
-            for task in others.get(r, []):
-                task()
+                convolve(r - 1)
+            finish_filler(r)
+            if r >= 2:
+                for block in finished[r - 2]:
+                    project(steps[r - 2][0], block)

@@ -70,6 +70,7 @@ def tile_multiheadattention820_pa_kernel(tc, v, attn_out, dyn_w, dyn_b, out_proj
         stage = ctx.enter_context(tc.tile_pool(name="stage", bufs=2))
         vq_pool = ctx.enter_context(tc.tile_pool(name="vq", bufs=2))
         soft = ctx.enter_context(tc.tile_pool(name="soft", bufs=2))
+        runs_pool = ctx.enter_context(tc.tile_pool(name="runs", bufs=3))
         skew_pool = ctx.enter_context(tc.tile_pool(name="skew", bufs=2))
         win_pool = ctx.enter_context(tc.tile_pool(name="win", bufs=4))
         wide_pool = ctx.enter_context(tc.tile_pool(name="wide", bufs=3))
@@ -201,21 +202,21 @@ def tile_multiheadattention820_pa_kernel(tc, v, attn_out, dyn_w, dyn_b, out_proj
         attn_parts = {}
         conv_parts = {}
 
-        def new_job(raw, blocks, codes, scales, pass_cols, of_chunk=False):
+        def new_job(raw, blocks, codes, scales, first_col=0, of_chunk=False):
             grouped = stage.tile([P, 2 * ROWS * PACK], BF16, align_bytes=64)
-            return (raw, blocks, codes, scales, pass_cols, of_chunk, grouped)
+            return (raw, blocks, codes, scales, first_col, of_chunk, grouped)
 
         def flip_block(job, n):
-            raw, blocks, codes, scales, pass_cols, of_chunk, grouped = job
+            raw, blocks, codes, scales, first_col, of_chunk, grouped = job
             words = raw[:].bitcast(F32)
-            grouped_words = grouped[:].bitcast(F32).rearrange("p (g r u) -> p g r u", g=2, u=2)
+            grouped_words = grouped[:, 0 : 2 * blocks * P * PACK].bitcast(F32).rearrange("p (g r u) -> p g r u", g=2, u=2)
             flipped = flip_psum.tile([P, 4 * P], F32, tag="flip")
             order = permuted[blocks] if of_chunk else ident_f32
             for gu in range(4):
                 first = n * WORDS + gu * P
                 nc.tensor.transpose(flipped[:, gu * P : (gu + 1) * P], words[:, first : first + P], order[:])
             if of_chunk:
-                to = grouped_words[:, :, 0 : blocks * P, :].rearrange("p g (m n q) u -> p n g m q u", m=TAPS, n=blocks)
+                to = grouped_words.rearrange("p g (m n q) u -> p n g m q u", m=TAPS, n=blocks)
                 nc.scalar.copy(
                     out=to[:, blocks - 1 - n],
                     in_=flipped[:].rearrange("p (g u m q) -> p g m q u", g=2, u=2, m=TAPS),
@@ -227,15 +228,11 @@ def tile_multiheadattention820_pa_kernel(tc, v, attn_out, dyn_w, dyn_b, out_proj
                 )
 
         def quantise_job(job):
-            raw, blocks, codes, scales, pass_cols, of_chunk, grouped = job
-            rows = blocks * P
-            for g in range(2):
-                cols = slice(pass_cols[g], pass_cols[g] + rows)
-                nc.vector.quantize_mx(
-                    out=codes[:, cols].bitcast(FP8X4),
-                    scales=scales[:, cols],
-                    in_=grouped[:, g * ROWS * PACK : g * ROWS * PACK + rows * PACK],
-                )
+            raw, blocks, codes, scales, first_col, of_chunk, grouped = job
+            cols = slice(first_col, first_col + 2 * blocks * P)
+            nc.vector.quantize_mx(
+                out=codes[:, cols].bitcast(FP8X4), scales=scales[:, cols], in_=grouped[:, 0 : 2 * blocks * P * PACK]
+            )
 
         def flip_blocks(job, first, count):
             for n in range(first, first + count):
@@ -243,50 +240,25 @@ def tile_multiheadattention820_pa_kernel(tc, v, attn_out, dyn_w, dyn_b, out_proj
             if first + count == job[1]:
                 quantise_job(job)
 
-        def softmax_over_taps(logits, final):
-            groups = 2 * H
-            weights = soft.tile([P, 2 * HK], F32)
-            by_head = weights[:].rearrange("p (m k) -> p m k", k=TAPS)
-            nc.vector.tensor_tensor(
-                out=weights[:].rearrange("p (n c) -> p n c", n=2),
-                in0=logits[:].rearrange("p (n c) -> p n c", n=2),
-                in1=dyn_b_f32[:].unsqueeze(1).to_broadcast([P, 2, HK]),
-                op=ALU.add,
-            )
-            top = soft.tile([P, groups], F32)
-            nc.vector.tensor_reduce(out=top[:], in_=by_head, axis=AXIS.X, op=ALU.max)
-            nc.vector.tensor_tensor(
-                out=by_head, in0=by_head, in1=top[:].unsqueeze(2).to_broadcast([P, groups, TAPS]), op=ALU.subtract
-            )
-            nc.scalar.activation(out=weights[:], in_=weights[:], func=ACT.Exp)
-            total = soft.tile([P, groups], F32)
-            nc.vector.tensor_reduce(out=total[:], in_=by_head, axis=AXIS.X, op=ALU.add)
-            inverse = soft.tile([P, groups], F32)
-            nc.vector.reciprocal(out=inverse[:], in_=total[:])
-            nc.vector.tensor_tensor(
-                out=final,
-                in0=weights[:].rearrange("p (n h k) -> p h n k", n=2, k=TAPS),
-                in1=inverse[:].rearrange("p (n h) -> p h n", n=2).unsqueeze(3).to_broadcast([P, H, 2, TAPS]),
-                op=ALU.mult,
-            )
-
 
         def chunk_job(c, raw):
             v_codes = vq_pool.tile([P, 2 * ROWS], U32, align_bytes=64)
             v_scales = vq_pool.tile([P, 2 * ROWS], U8, align_bytes=64)
-            return new_job(raw, CHUNKS[c][2], v_codes, v_scales, [0, ROWS], of_chunk=True)
+            return new_job(raw, CHUNKS[c][2], v_codes, v_scales, of_chunk=True)
+
+        exponents = {}
 
         def logits_chunk(c, job):
-            b, t0, blocks = CHUNKS[c]
+            blocks = CHUNKS[c][2]
             v_codes, v_scales = job[2], job[3]
-            run = blocks * TAPS
-            runs = soft.tile([P, UNITS * HK], F32)
-            by_block = runs[:, 0 : blocks * HK].rearrange("p (h j k) -> p h j k", h=H, k=TAPS)
+            runs = runs_pool.tile([P, UNITS * HK], F32)
+            by_block = runs[:, 0 : blocks * HK].rearrange("p (h j k) -> p j h k", h=H, k=TAPS)
             for pair in range(blocks // 2):
                 logits = acc_psum.tile([P, N_TILE], F32, tag="acc")
                 for n in range(2):
                     for g in range(2):
-                        cols = slice(g * ROWS + (2 * pair + n) * P, g * ROWS + (2 * pair + n + 1) * P)
+                        first = (g * blocks + 2 * pair + n) * P
+                        cols = slice(first, first + P)
                         nc.tensor.matmul_mx(
                             out=logits[:, n * HK : (n + 1) * HK],
                             lhsT=v_codes[:, cols].bitcast(FP8X4),
@@ -296,7 +268,35 @@ def tile_multiheadattention820_pa_kernel(tc, v, attn_out, dyn_w, dyn_b, out_proj
                             start=(g == 0),
                             stop=(g == 1),
                         )
-                softmax_over_taps(logits, by_block[:, :, 2 * pair : 2 * pair + 2, :])
+                nc.vector.tensor_tensor(
+                    out=by_block[:, 2 * pair : 2 * pair + 2],
+                    in0=logits[:].rearrange("p (n h k) -> p n h k", n=2, k=TAPS),
+                    in1=dyn_b_f32[:].rearrange("p (h k) -> p h k", k=TAPS).unsqueeze(1).to_broadcast([P, 2, H, TAPS]),
+                    op=ALU.add,
+                )
+            groups = blocks * H
+            by_group = runs[:, 0 : blocks * HK].rearrange("p (m k) -> p m k", k=TAPS)
+            top = soft.tile([P, UNITS * H], F32)
+            nc.vector.tensor_reduce(out=top[:, 0:groups], in_=by_group, axis=AXIS.X, op=ALU.max)
+            nc.vector.tensor_tensor(
+                out=by_group, in0=by_group, in1=top[:, 0:groups].unsqueeze(2).to_broadcast([P, groups, TAPS]), op=ALU.subtract
+            )
+            exponents[c] = runs
+
+        def weights_chunk(c):
+            b, t0, blocks = CHUNKS[c]
+            run = blocks * TAPS
+            runs = exponents[c]
+            groups = blocks * H
+            nc.scalar.activation(out=runs[:, 0 : blocks * HK], in_=runs[:, 0 : blocks * HK], func=ACT.Exp)
+            by_group = runs[:, 0 : blocks * HK].rearrange("p (m k) -> p m k", k=TAPS)
+            total = soft.tile([P, UNITS * H], F32)
+            nc.vector.tensor_reduce(out=total[:, 0:groups], in_=by_group, axis=AXIS.X, op=ALU.add)
+            inverse = soft.tile([P, UNITS * H], F32)
+            nc.vector.reciprocal(out=inverse[:, 0:groups], in_=total[:, 0:groups])
+            nc.vector.tensor_tensor(
+                out=by_group, in0=by_group, in1=inverse[:, 0:groups].unsqueeze(2).to_broadcast([P, groups, TAPS]), op=ALU.mult
+            )
             def to_scratch(start, row, parts, first, words):
                 pitch = region_words(row) // H
                 by_head = scratch[start : start + H * pitch].rearrange("(h z) -> h z", z=pitch)[:, TAPS:pitch]
@@ -319,13 +319,15 @@ def tile_multiheadattention820_pa_kernel(tc, v, attn_out, dyn_w, dyn_b, out_proj
             taps_f32 = keep.tile([P, T], F32, name="taps_f32%d" % b)
             skewed.append((taps_hi, taps_lo, taps_f32))
 
+        read_back = {}
+
         def read_skewed(c):
             b, t0, blocks = CHUNKS[c]
             end = t0 + blocks * P
             pieces = [(REGION_START[c], blocks * P, t0, 0 if t0 == 0 else t0 + PAD_L, T if end == T else end - PAD_L)]
             if t0 > 0:
                 pieces = [(EDGE_START[c - 1], EDGE_ROW, t0 - TAPS, t0 - PAD_L, t0 + PAD_L)] + pieces
-            taps_hi, taps_lo, taps_f32 = skewed[b]
+            taps_f32 = skewed[b][2]
             skew = skew_pool.tile([P, ROWS + TAPS], F32)
             first_col = pieces[0][3]
             last_col = pieces[-1][4]
@@ -337,8 +339,11 @@ def tile_multiheadattention820_pa_kernel(tc, v, attn_out, dyn_w, dyn_b, out_proj
                         out=into,
                         in_=scratch[first : first + P * (row + 1)].rearrange("(p y) -> p y", y=row + 1)[:, lo - origin : hi - origin],
                     )
-            first_heads = skew[:, 0 : last_col - first_col]
-            cols = slice(first_col, last_col)
+            read_back[c] = (skew[:, 0 : last_col - first_col], slice(first_col, last_col))
+
+        def split_skewed(c):
+            first_heads, cols = read_back[c]
+            taps_hi, taps_lo, taps_f32 = skewed[CHUNKS[c][0]]
             nc.scalar.copy(out=taps_hi[:, cols], in_=first_heads)
             nc.vector.tensor_tensor(out=taps_lo[:, cols], in0=first_heads, in1=taps_hi[:, cols], op=ALU.subtract)
 
@@ -462,13 +467,13 @@ def tile_multiheadattention820_pa_kernel(tc, v, attn_out, dyn_w, dyn_b, out_proj
 
         def project(b, block):
             quarter, tok = divmod(b * T + block * P, ROWS)
-            result = out_pool.tile([P, E], F32)
+            result = out_pool.tile([P, E], F32, tag="result")
             for nh in range(E // N_TILE):
                 acc = acc_psum.tile([P, N_TILE], F32, tag="acc")
                 for c in range(4):
                     codes, scales = attn_parts[quarter] if c < 2 else conv_parts[quarter]
                     cols = slice((c % 2) * ROWS + tok, (c % 2) * ROWS + tok + P)
-                    outs = slice(c * E + nh * N_TILE, c * E + (nh + 1) * N_TILE)
+                    outs = slice((nh * 4 + c) * N_TILE, (nh * 4 + c + 1) * N_TILE)
                     nc.tensor.matmul_mx(
                         out=acc[:],
                         lhsT=codes[:, cols].bitcast(FP8X4),
@@ -487,90 +492,94 @@ def tile_multiheadattention820_pa_kernel(tc, v, attn_out, dyn_w, dyn_b, out_proj
             nc.sync.dma_start(out=out_rows[:, block, b, :], in_=result[:])
 
         def w_job(nh, part, raw):
-            pass_cols = [(2 * part + g) * E + nh * N_TILE for g in range(2)]
-            return new_job(raw, UNITS, w_codes, w_scales, pass_cols)
+            return new_job(raw, UNITS, w_codes, w_scales, (nh * 4 + 2 * part) * N_TILE)
 
         def attn_job(quarter, raw_a):
             a_codes = keep.tile([P, 2 * ROWS], U32, align_bytes=64, name="a_codes%d" % quarter)
             a_scales = keep.tile([P, 2 * ROWS], U8, align_bytes=64, name="a_scales%d" % quarter)
             attn_parts[quarter] = (a_codes, a_scales)
-            return new_job(raw_a, UNITS, a_codes, a_scales, [0, ROWS])
+            return new_job(raw_a, UNITS, a_codes, a_scales)
 
-        ctx.enter_context(tc.manual_schedule(engines={mybir.EngineType.PE}))
+        ctx.enter_context(tc.manual_schedule(engines={mybir.EngineType.PE, mybir.EngineType.Activation}))
 
-        flip_blocks(new_job(raw_d, 2, d_codes, d_scales, [0, HK]), 0, 2)
         jobs = {}
-        jobs["c0"] = chunk_job(0, raw_v0)
-        flip_blocks(jobs["c0"], 0, 2)
-        jobs["c1"] = chunk_job(1, raw_v1)
-        flip_blocks(jobs["c1"], 0, 2)
-        logits_chunk(0, jobs["c0"])
+
+        flip_blocks(new_job(raw_d, 2, d_codes, d_scales), 0, 2)
+        chunk_jobs = [chunk_job(0, raw_v0), chunk_job(1, raw_v1)]
+        flip_blocks(chunk_jobs[0], 0, 2)
+        flip_blocks(chunk_jobs[1], 0, 2)
+        logits_chunk(0, chunk_jobs[0])
+        chunk_jobs.append(chunk_job(2, raw_v2))
+        flip_blocks(chunk_jobs[2], 0, 2)
+        logits_chunk(1, chunk_jobs[1])
+        weights_chunk(0)
         read_skewed(0)
-        jobs["c2"] = chunk_job(2, raw_v2)
-        flip_blocks(jobs["c2"], 0, 2)
-        logits_chunk(1, jobs["c1"])
+        flip_blocks(chunk_jobs[2], 2, 2)
+        weights_chunk(1)
         read_skewed(1)
-        flip_blocks(jobs["c2"], 2, 2)
         flip_blocks(w_job(0, 0, raw_w[(0, 0)]), 0, UNITS)
-        logits_chunk(2, jobs["c2"])
-        read_skewed(2)
+        logits_chunk(2, chunk_jobs[2])
         flip_blocks(w_job(0, 1, raw_w[(0, 1)]), 0, UNITS)
-        out_b_bf16 = consts.tile([P, E], BF16)
+        weights_chunk(2)
+        read_skewed(2)
+        flip_blocks(w_job(1, 0, raw_w[(1, 0)]), 0, UNITS)
+        split_skewed(0)
+        flip_blocks(w_job(1, 1, raw_w[(1, 1)]), 0, UNITS)
+        split_skewed(1)
+        flip_blocks(attn_job(0, raw_a0), 0, UNITS)
+        out_b_bf16 = out_pool.tile([P, E], BF16, tag="result")
         nc.sync.dma_start(out=out_b_bf16[:], in_=out_proj_b.partition_broadcast(P))
         out_b_f32 = consts.tile([P, E], F32)
         nc.vector.tensor_copy(out=out_b_f32[:], in_=out_b_bf16[:])
 
         fillers = {
-            0: ("w", (1, 0), 0, 4),
-            1: ("w", (1, 1), 0, 4),
-            2: ("a", 0, 0, 4),
-            3: ("c", 3, 0, 2),
-            4: ("c", 3, 2, 2),
-            5: ("a", 1, 0, 2),
-            6: ("a", 1, 2, 2),
-            7: ("c", 4, 0, 2),
-            8: ("c", 4, 2, 2),
-            9: ("a", 2, 0, 2),
-            10: ("a", 2, 2, 2),
-            11: ("a", 3, 0, 2),
-            12: ("a", 3, 2, 2),
+            1: ("c", 3, 0), 2: ("c", 3, 2), 3: ("a", 1, 0), 4: ("a", 1, 2), 5: ("c", 4, 0), 6: ("c", 4, 2),
+            7: ("a", 2, 0), 8: ("a", 2, 2), 9: ("a", 3, 0), 10: ("a", 3, 2),
         }
-        raws = {("w", (1, 0)): raw_w[(1, 0)], ("w", (1, 1)): raw_w[(1, 1)], ("a", 0): raw_a0}
+        raws = {}
 
         def load_filler(r):
-            kind, number, first, count = fillers.get(r, ("", 0, 1, 0))
-            if first == 0 and (kind, number) not in raws:
+            kind, number, first = fillers.get(r, ("", 0, 1))
+            if first == 0:
                 raws[(kind, number)] = load_chunk(number) if kind == "c" else load_attn(number)
 
         def flip_filler(r):
-            kind, number, first, count = fillers.get(r, ("", 0, 0, 0))
-            if count > 0:
+            kind, number, first = fillers.get(r, ("", 0, 0))
+            if kind != "":
                 if first == 0:
-                    make = {"w": lambda m, raw: w_job(m[0], m[1], raw), "a": attn_job, "c": chunk_job}[kind]
-                    jobs[(kind, number)] = make(number, raws[(kind, number)])
-                flip_blocks(jobs[(kind, number)], first, count)
+                    jobs[(kind, number)] = (chunk_job if kind == "c" else attn_job)(number, raws[(kind, number)])
+                flip_blocks(jobs[(kind, number)], first, 2)
 
-        def finish_filler(r):
-            kind, number, first, count = fillers.get(r, ("", 0, 0, 0))
-            if kind == "c" and first + count == UNITS:
-                logits_chunk(number, jobs[(kind, number)])
-                read_skewed(number)
+        def chunk_of(r):
+            kind, number, first = fillers.get(r, ("", 0, 0))
+            return [number] if kind == "c" and first > 0 else []
 
         n_steps = len(steps)
-        for r in range(n_steps + 2):
+        load_filler(1)
+        widen_window(0)
+        for r in range(n_steps + 3):
             if WINDOWS_AHEAD <= r + 1 < n_steps:
                 fetch_window(r + 1)
             load_filler(r + 2)
             if r < n_steps:
                 make_band(r)
-                widen_window(r)
-            if r >= 2:
+            if r == 0:
+                split_skewed(2)
+            for c in chunk_of(r - 1):
+                weights_chunk(c)
+                read_skewed(c)
+            if 2 <= r < n_steps + 2:
                 flip_conv(r - 2)
                 quantise_conv(r - 2)
             flip_filler(r)
+            for c in chunk_of(r - 3):
+                split_skewed(c)
             if 1 <= r < n_steps + 1:
                 convolve(r - 1)
-            finish_filler(r)
-            if r >= 2:
-                for block in finished[r - 2]:
-                    project(steps[r - 2][0], block)
+            if r + 1 < n_steps:
+                widen_window(r + 1)
+            for c in chunk_of(r):
+                logits_chunk(c, jobs[("c", c)])
+            if r >= 3:
+                for block in finished[r - 3]:
+                    project(steps[r - 3][0], block)

@@ -389,47 +389,52 @@ def tile_multiheadattention820_pa_kernel(tc, v, attn_out, dyn_w, dyn_b, out_proj
             runs = MIDDLE_RUNS if 0 < w < N_WINDOWS - 1 else P // TAPS
             extra = EXTRAS[w]
             wide = extra * TAPS
-            taps_pair = wide_pool.tile([P, 2 * P], BF16)
-            nc.scalar.copy(out=taps_pair[:], in_=by_time_bf16)
-            taps_rest = wide_pool.tile([P, P], F32)
-            nc.scalar.copy(out=taps_rest[:], in_=by_time[:, P : 2 * P])
+            taps_rest = by_time[:, P : 2 * P]
             taps_extra = wide_pool.tile([P, 2 * MAX_EXTRA * TAPS], BF16)
             nc.scalar.copy(out=taps_extra[:, 0:wide], in_=taps_rest[:, 0:wide])
-            banded(band_pair[:], taps_pair[:], swapped_mask_bf16[:], 2 * PAIR_HEADS, runs)
+            banded(band_pair[:], by_time_bf16, swapped_mask_bf16[:], 2 * PAIR_HEADS, runs)
             nc.vector.tensor_tensor(
                 out=taps_extra[:, wide : 2 * wide], in0=taps_rest[:, 0:wide], in1=taps_extra[:, 0:wide], op=ALU.subtract
             )
             banded(band_f32[:, 0 : (PAIR_HEADS - extra) * P], taps_rest[:, wide:P], swapped_mask[:], PAIR_HEADS - extra, runs)
             banded(band_extra[:, 0 : 2 * extra * P], taps_extra[:, 0 : 2 * wide], swapped_mask_bf16[:], 2 * extra, runs)
 
-        def convolve(s):
+        def start_convolution(s):
             window_bf16, window_f32 = windows[s], wide_windows[s]
             band_pair, band_extra, band_f32 = bands[s % BAND_SETS]
             extra = EXTRAS[steps[s][1]]
             conv_bf16 = conv_pool.tile([P, E], BF16)
+            conv_tiles[s] = conv_bf16
+            sums = []
             for g in range(2):
                 conv_f32 = conv_psum.tile([P, K_PASS], F32, tag="conv")
-                for hl in range(HEADS_PER_PASS):
-                    sums = conv_f32[:, hl * R : (hl + 1) * R]
+                sums.append(conv_f32)
+                band, in_pairs = ((band_pair, PAIR_HEADS), (band_extra, extra))[g]
+                for hl in range(in_pairs):
                     h = g * HEADS_PER_PASS + hl
-                    in_pairs = PAIR_HEADS if g == 0 else extra
-                    if hl < in_pairs:
-                        band = band_pair if g == 0 else band_extra
-                        for part in range(2):
-                            m = part * in_pairs + hl
-                            nc.tensor.matmul(
-                                out=sums, lhsT=band[:, m * P : (m + 1) * P], rhs=window_bf16[:, h * R : (h + 1) * R],
-                                start=(part == 0), stop=(part == 1),
-                            )
-                    else:
-                        m = hl - extra
-                        f = h - (H - F32_HEADS)
+                    for part in range(2):
+                        m = part * in_pairs + hl
                         nc.tensor.matmul(
-                            out=sums, lhsT=band_f32[:, m * P : (m + 1) * P], rhs=window_f32[:, f * R : (f + 1) * R],
-                            start=True, stop=True,
+                            out=conv_f32[:, hl * R : (hl + 1) * R],
+                            lhsT=band[:, m * P : (m + 1) * P], rhs=window_bf16[:, h * R : (h + 1) * R],
+                            start=(part == 0), stop=(part == 1),
                         )
-                nc.scalar.copy(out=conv_bf16[:, g * K_PASS : (g + 1) * K_PASS], in_=conv_f32[:])
-            conv_tiles[s] = conv_bf16
+                if g == 0:
+                    nc.scalar.copy(out=conv_bf16[:, 0:K_PASS], in_=conv_f32[:])
+
+            def f32_head(hl):
+                m = hl - extra
+                f = HEADS_PER_PASS + hl - (H - F32_HEADS)
+                nc.tensor.matmul(
+                    out=sums[1][:, hl * R : (hl + 1) * R],
+                    lhsT=band_f32[:, m * P : (m + 1) * P], rhs=window_f32[:, f * R : (f + 1) * R],
+                    start=True, stop=True,
+                )
+
+            def finish():
+                nc.scalar.copy(out=conv_bf16[:, K_PASS:E], in_=sums[1][:])
+
+            return [lambda hl=hl: f32_head(hl) for hl in range(extra, HEADS_PER_PASS)] + [finish]
 
         def flip_conv(s):
             w = steps[s][1]
@@ -465,31 +470,35 @@ def tile_multiheadattention820_pa_kernel(tc, v, attn_out, dyn_w, dyn_b, out_proj
                         out=c_codes[:, cols].bitcast(FP8X4), scales=c_scales[:, cols], in_=grouped_conv[:, first : first + P * PACK]
                     )
 
-        def project(b, block):
+        def projection(b, block):
             quarter, tok = divmod(b * T + block * P, ROWS)
             result = out_pool.tile([P, E], F32, tag="result")
-            for nh in range(E // N_TILE):
-                acc = acc_psum.tile([P, N_TILE], F32, tag="acc")
-                for c in range(4):
-                    codes, scales = attn_parts[quarter] if c < 2 else conv_parts[quarter]
-                    cols = slice((c % 2) * ROWS + tok, (c % 2) * ROWS + tok + P)
-                    outs = slice((nh * 4 + c) * N_TILE, (nh * 4 + c + 1) * N_TILE)
-                    nc.tensor.matmul_mx(
-                        out=acc[:],
-                        lhsT=codes[:, cols].bitcast(FP8X4),
-                        lhsT_scale=scales[:, cols],
-                        rhs=w_codes[:, outs].bitcast(FP8X4),
-                        rhs_scale=w_scales[:, outs],
-                        start=(c == 0),
-                        stop=(c == 3),
-                    )
-                nc.vector.tensor_tensor(
-                    out=result[:, nh * N_TILE : (nh + 1) * N_TILE],
-                    in0=acc[:],
-                    in1=out_b_f32[:, nh * N_TILE : (nh + 1) * N_TILE],
-                    op=ALU.add,
+            accs = {}
+
+            def one_pass(nh, c):
+                if c == 0:
+                    acc = acc_psum.tile([P, N_TILE], F32, tag="acc")
+                    accs[nh] = acc
+                acc = accs[nh]
+                codes, scales = attn_parts[quarter] if c < 2 else conv_parts[quarter]
+                cols = slice((c % 2) * ROWS + tok, (c % 2) * ROWS + tok + P)
+                outs = slice((nh * 4 + c) * N_TILE, (nh * 4 + c + 1) * N_TILE)
+                nc.tensor.matmul_mx(
+                    out=acc[:],
+                    lhsT=codes[:, cols].bitcast(FP8X4),
+                    lhsT_scale=scales[:, cols],
+                    rhs=w_codes[:, outs].bitcast(FP8X4),
+                    rhs_scale=w_scales[:, outs],
+                    start=(c == 0),
+                    stop=(c == 3),
                 )
-            nc.sync.dma_start(out=out_rows[:, block, b, :], in_=result[:])
+                if c == 3:
+                    cols_out = slice(nh * N_TILE, (nh + 1) * N_TILE)
+                    nc.vector.tensor_tensor(out=result[:, cols_out], in0=acc[:], in1=out_b_f32[:, cols_out], op=ALU.add)
+                    if nh == 1:
+                        nc.sync.dma_start(out=out_rows[:, block, b, :], in_=result[:])
+
+            return [lambda nh=nh, c=c: one_pass(nh, c) for nh in range(E // N_TILE) for c in range(4)]
 
         def w_job(nh, part, raw):
             return new_job(raw, UNITS, w_codes, w_scales, (nh * 4 + 2 * part) * N_TILE)
@@ -568,18 +577,24 @@ def tile_multiheadattention820_pa_kernel(tc, v, attn_out, dyn_w, dyn_b, out_proj
             for c in chunk_of(r - 1):
                 weights_chunk(c)
                 read_skewed(c)
+            flip_filler(r)
             if 2 <= r < n_steps + 2:
                 flip_conv(r - 2)
                 quantise_conv(r - 2)
-            flip_filler(r)
             for c in chunk_of(r - 3):
                 split_skewed(c)
+            wide = []
             if 1 <= r < n_steps + 1:
-                convolve(r - 1)
+                wide = start_convolution(r - 1)
             if r + 1 < n_steps:
                 widen_window(r + 1)
             for c in chunk_of(r):
                 logits_chunk(c, jobs[("c", c)])
+            passes = []
             if r >= 3:
                 for block in finished[r - 3]:
-                    project(steps[r - 3][0], block)
+                    passes = passes + projection(steps[r - 3][0], block)
+            for n in range(max(len(wide), len(passes))):
+                for calls in (wide, passes):
+                    if n < len(calls):
+                        calls[n]()

@@ -495,10 +495,17 @@ def tile_multiheadattention820_pa_kernel(tc, v, attn_out, dyn_w, dyn_b, out_proj
                 if c == 3:
                     cols_out = slice(nh * N_TILE, (nh + 1) * N_TILE)
                     nc.vector.tensor_tensor(out=result[:, cols_out], in0=acc[:], in1=out_b_f32[:, cols_out], op=ALU.add)
-                    if nh == 1:
+                    if last:
+                        nc.sync.dma_start(out=out_rows[:, block, b, cols_out], in_=result[:, cols_out])
+                    elif nh == 1:
                         nc.sync.dma_start(out=out_rows[:, block, b, :], in_=result[:])
 
-            return [lambda nh=nh, c=c: one_pass(nh, c) for nh in range(E // N_TILE) for c in range(4)]
+            last = b == B - 1 and block == T // P - 1
+            halves = range(E // N_TILE)
+            order = [(nh, c) for nh in halves for c in range(4)]
+            if last:
+                order = [(nh, c) for c in range(2) for nh in halves] + [(nh, c) for nh in halves for c in range(2, 4)]
+            return [lambda nh=nh, c=c: one_pass(nh, c) for nh, c in order]
 
         def w_job(nh, part, raw):
             return new_job(raw, UNITS, w_codes, w_scales, (nh * 4 + 2 * part) * N_TILE)
@@ -529,22 +536,23 @@ def tile_multiheadattention820_pa_kernel(tc, v, attn_out, dyn_w, dyn_b, out_proj
         flip_blocks(w_job(0, 0, raw_w[(0, 0)]), 0, UNITS)
         logits_chunk(2, chunk_jobs[2])
         flip_blocks(w_job(0, 1, raw_w[(0, 1)]), 0, UNITS)
-        weights_chunk(2)
-        read_skewed(2)
         flip_blocks(w_job(1, 0, raw_w[(1, 0)]), 0, UNITS)
         split_skewed(0)
         flip_blocks(w_job(1, 1, raw_w[(1, 1)]), 0, UNITS)
         split_skewed(1)
         flip_blocks(attn_job(0, raw_a0), 0, UNITS)
+        weights_chunk(2)
+        read_skewed(2)
         out_b_bf16 = out_pool.tile([P, E], BF16, tag="result")
         nc.sync.dma_start(out=out_b_bf16[:], in_=out_proj_b.partition_broadcast(P))
         out_b_f32 = consts.tile([P, E], F32)
         nc.vector.tensor_copy(out=out_b_f32[:], in_=out_b_bf16[:])
 
         fillers = {
-            1: ("c", 3, 0), 2: ("c", 3, 2), 3: ("a", 1, 0), 4: ("a", 1, 2), 5: ("c", 4, 0), 6: ("c", 4, 2),
-            7: ("a", 2, 0), 8: ("a", 2, 2), 9: ("a", 3, 0), 10: ("a", 3, 2),
+            2: ("c", 3, 0), 3: ("c", 3, 2), 4: ("a", 1, 0), 5: ("a", 1, 2), 6: ("c", 4, 0), 7: ("c", 4, 2),
+            8: ("a", 2, 0), 9: ("a", 2, 2), 10: ("a", 3, 0), 11: ("a", 3, 2),
         }
+        chunk_rounds = {2: (-1, -1, 3), 3: (4, 5, 7), 4: (8, 9, 11)}
         raws = {}
 
         def load_filler(r):
@@ -559,37 +567,32 @@ def tile_multiheadattention820_pa_kernel(tc, v, attn_out, dyn_w, dyn_b, out_proj
                     jobs[(kind, number)] = (chunk_job if kind == "c" else attn_job)(number, raws[(kind, number)])
                 flip_blocks(jobs[(kind, number)], first, 2)
 
-        def chunk_of(r):
-            kind, number, first = fillers.get(r, ("", 0, 0))
-            return [number] if kind == "c" and first > 0 else []
-
         n_steps = len(steps)
-        load_filler(1)
         widen_window(0)
         for r in range(n_steps + 3):
             if WINDOWS_AHEAD <= r + 1 < n_steps:
                 fetch_window(r + 1)
-            load_filler(r + 2)
+            load_filler(r + 1)
             if r < n_steps:
                 make_band(r)
-            if r == 0:
-                split_skewed(2)
-            for c in chunk_of(r - 1):
-                weights_chunk(c)
-                read_skewed(c)
             flip_filler(r)
             if 2 <= r < n_steps + 2:
                 flip_conv(r - 2)
                 quantise_conv(r - 2)
-            for c in chunk_of(r - 3):
-                split_skewed(c)
+            for c in chunk_rounds:
+                if r == chunk_rounds[c][1]:
+                    weights_chunk(c)
+                    read_skewed(c)
+                if r == chunk_rounds[c][2]:
+                    split_skewed(c)
             wide = []
             if 1 <= r < n_steps + 1:
                 wide = start_convolution(r - 1)
             if r + 1 < n_steps:
                 widen_window(r + 1)
-            for c in chunk_of(r):
-                logits_chunk(c, jobs[("c", c)])
+            for c in chunk_rounds:
+                if r == chunk_rounds[c][0]:
+                    logits_chunk(c, jobs[("c", c)])
             passes = []
             if r >= 3:
                 for block in finished[r - 3]:

@@ -50,11 +50,12 @@ SCRATCH_WORDS = EDGE_START[-1] + EDGE_WORDS + region_words(UNITS * P) // H
 
 HEADS_PER_PASS = K_PASS // R
 PAIR_HEADS = HEADS_PER_PASS
-MAX_EXTRA = 2
-EXTRAS = [MAX_EXTRA - w % 2 for w in range(N_WINDOWS)]
+EXTRA = 2
+NO_EXTRA = 4
+EXTRAS = [0 if s < NO_EXTRA else EXTRA for s in range(B * N_WINDOWS)]
 LIMIT_FLOPS = (2 * TOKENS * E * HK + 2 * TOKENS * (2 * E) * E) // 10
-assert B * sum(H + PAIR_HEADS + e for e in EXTRAS) * 2 * P * P * R <= LIMIT_FLOPS
-F32_HEADS = H - PAIR_HEADS - min(EXTRAS)
+assert sum(H + PAIR_HEADS + e for e in EXTRAS) * 2 * P * P * R <= LIMIT_FLOPS
+F32_HEADS = H - PAIR_HEADS
 WINDOWS_AHEAD = 2
 BAND_SETS = 3
 
@@ -119,8 +120,6 @@ def tile_multiheadattention820_pa_kernel(tc, v, attn_out, dyn_w, dyn_b, out_proj
 
         raw_v0 = load_chunk(0)
         raw_d = load_rows(dyn_rows)
-        dyn_b_bf16 = consts.tile([P, HK], BF16)
-        nc.sync.dma_start(out=dyn_b_bf16[:], in_=dyn_b.partition_broadcast(P))
         raw_v1 = load_chunk(1)
         raw_v2 = load_chunk(2)
         for s in range(WINDOWS_AHEAD):
@@ -163,8 +162,15 @@ def tile_multiheadattention820_pa_kernel(tc, v, attn_out, dyn_w, dyn_b, out_proj
         nc.vector.memset(warm[:], 0.0)
         nc.scalar.activation(out=warm[:], in_=warm[:], func=ACT.Exp)
 
+        bias_rows = consts.tile([P, P], BF16)
+        nc.vector.memset(bias_rows[:], 0.0)
+        nc.sync.dma_start(out=bias_rows[0 : HK // P, :], in_=dyn_b.rearrange("(n c) -> n c", c=P))
+        nc.sync.dma_start(out=bias_rows[HK // P : (HK + E) // P, :], in_=out_proj_b.rearrange("(n c) -> n c", c=P))
         dyn_b_f32 = consts.tile([P, HK], F32)
-        nc.vector.tensor_copy(out=dyn_b_f32[:], in_=dyn_b_bf16[:])
+        out_b_f32 = consts.tile([P, E], F32)
+        ident_bf16 = consts.tile([P, P], BF16)
+        nc.vector.tensor_copy(out=ident_bf16[:], in_=ident_f32[:])
+        bias_columns = consts.tile([P, (HK + E) // P], BF16)
 
         reversed_f32 = consts.tile([P, P], F32)
         by_tap = reversed_f32[:].rearrange("p (h i) -> p h i", i=TAPS)
@@ -283,12 +289,15 @@ def tile_multiheadattention820_pa_kernel(tc, v, attn_out, dyn_w, dyn_b, out_proj
             )
             exponents[c] = runs
 
+        def exponentials(c):
+            wide = CHUNKS[c][2] * HK
+            nc.scalar.activation(out=exponents[c][:, 0:wide], in_=exponents[c][:, 0:wide], func=ACT.Exp)
+
         def weights_chunk(c):
             b, t0, blocks = CHUNKS[c]
             run = blocks * TAPS
             runs = exponents[c]
             groups = blocks * H
-            nc.scalar.activation(out=runs[:, 0 : blocks * HK], in_=runs[:, 0 : blocks * HK], func=ACT.Exp)
             by_group = runs[:, 0 : blocks * HK].rearrange("p (m k) -> p m k", k=TAPS)
             total = soft.tile([P, UNITS * H], F32)
             nc.vector.tensor_reduce(out=total[:, 0:groups], in_=by_group, axis=AXIS.X, op=ALU.add)
@@ -351,7 +360,7 @@ def tile_multiheadattention820_pa_kernel(tc, v, attn_out, dyn_w, dyn_b, out_proj
         bands = []
         for n in range(BAND_SETS):
             band_pair = keep.tile([P, 2 * PAIR_HEADS * P], BF16, name="band_pair%d" % n)
-            band_extra = keep.tile([P, 2 * MAX_EXTRA * P], BF16, name="band_extra%d" % n)
+            band_extra = keep.tile([P, 2 * EXTRA * P], BF16, name="band_extra%d" % n)
             band_f32 = keep.tile([P, F32_HEADS * P], F32, name="band_f32%d" % n)
             for band in (band_pair, band_extra, band_f32):
                 nc.gpsimd.memset(band[:].rearrange("p (m x) -> p m x", x=P)[:, :, WINDOW_STEP:P], 0.0)
@@ -364,7 +373,8 @@ def tile_multiheadattention820_pa_kernel(tc, v, attn_out, dyn_w, dyn_b, out_proj
 
         def widen_window(s):
             window_f32 = wide_pool.tile([P, F32_HEADS * R], F32)
-            nc.scalar.copy(out=window_f32[:], in_=windows[s][:, E - F32_HEADS * R : E])
+            first = EXTRAS[s] * R
+            nc.scalar.copy(out=window_f32[:, first:], in_=windows[s][:, E - F32_HEADS * R + first : E])
             wide_windows[s] = window_f32
 
         def banded(band, taps, mask, matrices, runs):
@@ -387,22 +397,25 @@ def tile_multiheadattention820_pa_kernel(tc, v, attn_out, dyn_w, dyn_b, out_proj
             nc.tensor.transpose(by_time[:, P : 2 * P], taps_f32[:, t0 : t0 + P], reversed_f32[:])
             band_pair, band_extra, band_f32 = bands[s % BAND_SETS]
             runs = MIDDLE_RUNS if 0 < w < N_WINDOWS - 1 else P // TAPS
-            extra = EXTRAS[w]
+            extra = EXTRAS[s]
             wide = extra * TAPS
-            taps_rest = by_time[:, P : 2 * P]
-            taps_extra = wide_pool.tile([P, 2 * MAX_EXTRA * TAPS], BF16)
-            nc.scalar.copy(out=taps_extra[:, 0:wide], in_=taps_rest[:, 0:wide])
+            rest = by_time[:, P : 2 * P]
+            if extra > 0:
+                taps_extra = wide_pool.tile([P, 2 * EXTRA * TAPS], BF16)
+                nc.scalar.copy(out=taps_extra[:, 0:wide], in_=rest[:, 0:wide])
             banded(band_pair[:], by_time_bf16, swapped_mask_bf16[:], 2 * PAIR_HEADS, runs)
-            nc.vector.tensor_tensor(
-                out=taps_extra[:, wide : 2 * wide], in0=taps_rest[:, 0:wide], in1=taps_extra[:, 0:wide], op=ALU.subtract
-            )
-            banded(band_f32[:, 0 : (PAIR_HEADS - extra) * P], taps_rest[:, wide:P], swapped_mask[:], PAIR_HEADS - extra, runs)
-            banded(band_extra[:, 0 : 2 * extra * P], taps_extra[:, 0 : 2 * wide], swapped_mask_bf16[:], 2 * extra, runs)
+            if extra > 0:
+                nc.vector.tensor_tensor(
+                    out=taps_extra[:, wide : 2 * wide], in0=rest[:, 0:wide], in1=taps_extra[:, 0:wide], op=ALU.subtract
+                )
+            banded(band_f32[:, extra * P : F32_HEADS * P], rest[:, wide:P], swapped_mask[:], F32_HEADS - extra, runs)
+            if extra > 0:
+                banded(band_extra[:], taps_extra[:], swapped_mask_bf16[:], 2 * extra, runs)
 
         def start_convolution(s):
             window_bf16, window_f32 = windows[s], wide_windows[s]
             band_pair, band_extra, band_f32 = bands[s % BAND_SETS]
-            extra = EXTRAS[steps[s][1]]
+            extra = EXTRAS[s]
             conv_bf16 = conv_pool.tile([P, E], BF16)
             conv_tiles[s] = conv_bf16
             sums = []
@@ -423,11 +436,9 @@ def tile_multiheadattention820_pa_kernel(tc, v, attn_out, dyn_w, dyn_b, out_proj
                     nc.scalar.copy(out=conv_bf16[:, 0:K_PASS], in_=conv_f32[:])
 
             def f32_head(hl):
-                m = hl - extra
-                f = HEADS_PER_PASS + hl - (H - F32_HEADS)
                 nc.tensor.matmul(
                     out=sums[1][:, hl * R : (hl + 1) * R],
-                    lhsT=band_f32[:, m * P : (m + 1) * P], rhs=window_f32[:, f * R : (f + 1) * R],
+                    lhsT=band_f32[:, hl * P : (hl + 1) * P], rhs=window_f32[:, hl * R : (hl + 1) * R],
                     start=True, stop=True,
                 )
 
@@ -507,6 +518,12 @@ def tile_multiheadattention820_pa_kernel(tc, v, attn_out, dyn_w, dyn_b, out_proj
                 order = [(nh, c) for c in range(2) for nh in halves] + [(nh, c) for nh in halves for c in range(2, 4)]
             return [lambda nh=nh, c=c: one_pass(nh, c) for nh, c in order]
 
+        def projections(s):
+            calls = []
+            for block in finished[s]:
+                calls = calls + projection(steps[s][0], block)
+            return calls
+
         def w_job(nh, part, raw):
             return new_job(raw, UNITS, w_codes, w_scales, (nh * 4 + 2 * part) * N_TILE)
 
@@ -520,34 +537,46 @@ def tile_multiheadattention820_pa_kernel(tc, v, attn_out, dyn_w, dyn_b, out_proj
 
         jobs = {}
 
+        def spread_bias(bias, first):
+            width = bias.shape[1]
+            spread = flip_psum.tile([P, E], BF16, tag="flip")
+            for n in range(width // P):
+                column = bias_columns[:, first + n : first + n + 1]
+                nc.tensor.transpose(spread[:, n * P : (n + 1) * P], column.to_broadcast([P, P]), ident_bf16[:])
+            nc.scalar.copy(out=bias[:], in_=spread[:, 0:width])
+
         flip_blocks(new_job(raw_d, 2, d_codes, d_scales), 0, 2)
         chunk_jobs = [chunk_job(0, raw_v0), chunk_job(1, raw_v1)]
         flip_blocks(chunk_jobs[0], 0, 2)
         flip_blocks(chunk_jobs[1], 0, 2)
+        turned = flip_psum.tile([P, P], BF16, tag="flip")
+        nc.tensor.transpose(turned[:], bias_rows[:], ident_bf16[:])
+        nc.scalar.copy(out=bias_columns[:], in_=turned[:, 0 : (HK + E) // P])
+        spread_bias(dyn_b_f32, 0)
         logits_chunk(0, chunk_jobs[0])
         chunk_jobs.append(chunk_job(2, raw_v2))
         flip_blocks(chunk_jobs[2], 0, 2)
         logits_chunk(1, chunk_jobs[1])
+        exponentials(0)
         weights_chunk(0)
         read_skewed(0)
         flip_blocks(chunk_jobs[2], 2, 2)
+        exponentials(1)
         weights_chunk(1)
         read_skewed(1)
         flip_blocks(w_job(0, 0, raw_w[(0, 0)]), 0, UNITS)
         logits_chunk(2, chunk_jobs[2])
+        spread_bias(out_b_f32, HK // P)
         flip_blocks(w_job(0, 1, raw_w[(0, 1)]), 0, UNITS)
         flip_blocks(w_job(1, 0, raw_w[(1, 0)]), 0, UNITS)
         split_skewed(0)
         flip_blocks(w_job(1, 1, raw_w[(1, 1)]), 0, UNITS)
-        split_skewed(1)
-        flip_blocks(attn_job(0, raw_a0), 0, UNITS)
+        exponentials(2)
+        make_band(0)
         weights_chunk(2)
         read_skewed(2)
-        out_b_bf16 = out_pool.tile([P, E], BF16, tag="result")
-        nc.sync.dma_start(out=out_b_bf16[:], in_=out_proj_b.partition_broadcast(P))
-        out_b_f32 = consts.tile([P, E], F32)
-        nc.vector.tensor_copy(out=out_b_f32[:], in_=out_b_bf16[:])
-
+        split_skewed(1)
+        flip_blocks(attn_job(0, raw_a0), 0, UNITS)
         fillers = {
             2: ("c", 3, 0), 3: ("c", 3, 2), 4: ("a", 1, 0), 5: ("a", 1, 2), 6: ("c", 4, 0), 7: ("c", 4, 2),
             8: ("a", 2, 0), 9: ("a", 2, 2), 10: ("a", 3, 0), 11: ("a", 3, 2),
@@ -569,11 +598,12 @@ def tile_multiheadattention820_pa_kernel(tc, v, attn_out, dyn_w, dyn_b, out_proj
 
         n_steps = len(steps)
         widen_window(0)
-        for r in range(n_steps + 3):
+        late = []
+        for r in range(n_steps + 2):
             if WINDOWS_AHEAD <= r + 1 < n_steps:
                 fetch_window(r + 1)
             load_filler(r + 1)
-            if r < n_steps:
+            if 0 < r < n_steps:
                 make_band(r)
             flip_filler(r)
             if 2 <= r < n_steps + 2:
@@ -581,6 +611,7 @@ def tile_multiheadattention820_pa_kernel(tc, v, attn_out, dyn_w, dyn_b, out_proj
                 quantise_conv(r - 2)
             for c in chunk_rounds:
                 if r == chunk_rounds[c][1]:
+                    exponentials(c)
                     weights_chunk(c)
                     read_skewed(c)
                 if r == chunk_rounds[c][2]:
@@ -594,9 +625,13 @@ def tile_multiheadattention820_pa_kernel(tc, v, attn_out, dyn_w, dyn_b, out_proj
                 if r == chunk_rounds[c][0]:
                     logits_chunk(c, jobs[("c", c)])
             passes = []
-            if r >= 3:
-                for block in finished[r - 3]:
-                    passes = passes + projection(steps[r - 3][0], block)
+            if 3 <= r <= n_steps:
+                passes = projections(r - 3)
+            if r == n_steps:
+                late = projections(n_steps - 2)
+                passes = passes + late[0 : len(late) // 2]
+            if r == n_steps + 1:
+                passes = late[len(late) // 2 :] + projections(n_steps - 1)
             for n in range(max(len(wide), len(passes))):
                 for calls in (wide, passes):
                     if n < len(calls):

@@ -120,6 +120,10 @@ def tile_multiheadattention820_pa_kernel(tc, v, attn_out, dyn_w, dyn_b, out_proj
 
         raw_v0 = load_chunk(0)
         raw_d = load_rows(dyn_rows)
+        bias_rows = consts.tile([P, P], BF16)
+        nc.vector.memset(bias_rows[:], 0.0)
+        nc.sync.dma_start(out=bias_rows[0 : HK // P, :], in_=dyn_b.rearrange("(n c) -> n c", c=P))
+        nc.sync.dma_start(out=bias_rows[HK // P : (HK + E) // P, :], in_=out_proj_b.rearrange("(n c) -> n c", c=P))
         raw_v1 = load_chunk(1)
         raw_v2 = load_chunk(2)
         for s in range(WINDOWS_AHEAD):
@@ -162,10 +166,6 @@ def tile_multiheadattention820_pa_kernel(tc, v, attn_out, dyn_w, dyn_b, out_proj
         nc.vector.memset(warm[:], 0.0)
         nc.scalar.activation(out=warm[:], in_=warm[:], func=ACT.Exp)
 
-        bias_rows = consts.tile([P, P], BF16)
-        nc.vector.memset(bias_rows[:], 0.0)
-        nc.sync.dma_start(out=bias_rows[0 : HK // P, :], in_=dyn_b.rearrange("(n c) -> n c", c=P))
-        nc.sync.dma_start(out=bias_rows[HK // P : (HK + E) // P, :], in_=out_proj_b.rearrange("(n c) -> n c", c=P))
         dyn_b_f32 = consts.tile([P, HK], F32)
         out_b_f32 = consts.tile([P, E], F32)
         ident_bf16 = consts.tile([P, P], BF16)

@@ -254,6 +254,9 @@ def tile_multiheadattention820_pa_kernel(tc, v, attn_out, dyn_w, dyn_b, out_proj
 
         exponents = {}
 
+        def engine_of(c):
+            return nc.vector if CHUNKS[c][0] == 0 else nc.gpsimd
+
         def logits_chunk(c, job):
             blocks = CHUNKS[c][2]
             v_codes, v_scales = job[2], job[3]
@@ -284,7 +287,7 @@ def tile_multiheadattention820_pa_kernel(tc, v, attn_out, dyn_w, dyn_b, out_proj
             by_group = runs[:, 0 : blocks * HK].rearrange("p (m k) -> p m k", k=TAPS)
             top = soft.tile([P, UNITS * H], F32)
             nc.vector.tensor_reduce(out=top[:, 0:groups], in_=by_group, axis=AXIS.X, op=ALU.max)
-            nc.vector.tensor_tensor(
+            engine_of(c).tensor_tensor(
                 out=by_group, in0=by_group, in1=top[:, 0:groups].unsqueeze(2).to_broadcast([P, groups, TAPS]), op=ALU.subtract
             )
             exponents[c] = runs
@@ -303,7 +306,7 @@ def tile_multiheadattention820_pa_kernel(tc, v, attn_out, dyn_w, dyn_b, out_proj
             nc.vector.tensor_reduce(out=total[:, 0:groups], in_=by_group, axis=AXIS.X, op=ALU.add)
             inverse = soft.tile([P, UNITS * H], F32)
             nc.vector.reciprocal(out=inverse[:, 0:groups], in_=total[:, 0:groups])
-            nc.vector.tensor_tensor(
+            engine_of(c).tensor_tensor(
                 out=by_group, in0=by_group, in1=inverse[:, 0:groups].unsqueeze(2).to_broadcast([P, groups, TAPS]), op=ALU.mult
             )
             def to_scratch(start, row, parts, first, words):
@@ -354,7 +357,7 @@ def tile_multiheadattention820_pa_kernel(tc, v, attn_out, dyn_w, dyn_b, out_proj
             first_heads, cols = read_back[c]
             taps_hi, taps_lo, taps_f32 = skewed[CHUNKS[c][0]]
             nc.scalar.copy(out=taps_hi[:, cols], in_=first_heads)
-            nc.vector.tensor_tensor(out=taps_lo[:, cols], in0=first_heads, in1=taps_hi[:, cols], op=ALU.subtract)
+            nc.gpsimd.tensor_tensor(out=taps_lo[:, cols], in0=first_heads, in1=taps_hi[:, cols], op=ALU.subtract)
 
         wide_windows = {}
         bands = []
@@ -512,11 +515,7 @@ def tile_multiheadattention820_pa_kernel(tc, v, attn_out, dyn_w, dyn_b, out_proj
                         nc.sync.dma_start(out=out_rows[:, block, b, :], in_=result[:])
 
             last = b == B - 1 and block == T // P - 1
-            halves = range(E // N_TILE)
-            order = [(nh, c) for nh in halves for c in range(4)]
-            if last:
-                order = [(nh, c) for c in range(2) for nh in halves] + [(nh, c) for nh in halves for c in range(2, 4)]
-            return [lambda nh=nh, c=c: one_pass(nh, c) for nh, c in order]
+            return [lambda nh=nh, c=c: one_pass(nh, c) for nh in range(E // N_TILE) for c in range(4)]
 
         def projections(s):
             calls = []
@@ -566,7 +565,6 @@ def tile_multiheadattention820_pa_kernel(tc, v, attn_out, dyn_w, dyn_b, out_proj
         read_skewed(1)
         flip_blocks(w_job(0, 0, raw_w[(0, 0)]), 0, UNITS)
         logits_chunk(2, chunk_jobs[2])
-        spread_bias(out_b_f32, HK // P)
         flip_blocks(w_job(0, 1, raw_w[(0, 1)]), 0, UNITS)
         flip_blocks(w_job(1, 0, raw_w[(1, 0)]), 0, UNITS)
         split_skewed(0)
@@ -581,7 +579,7 @@ def tile_multiheadattention820_pa_kernel(tc, v, attn_out, dyn_w, dyn_b, out_proj
             2: ("c", 3, 0), 3: ("c", 3, 2), 4: ("a", 1, 0), 5: ("a", 1, 2), 6: ("c", 4, 0), 7: ("c", 4, 2),
             8: ("a", 2, 0), 9: ("a", 2, 2), 10: ("a", 3, 0), 11: ("a", 3, 2),
         }
-        chunk_rounds = {2: (-1, -1, 3), 3: (4, 5, 7), 4: (8, 9, 11)}
+        chunk_rounds = {2: (-1, -1, 3), 3: (4, 5, 8), 4: (8, 9, 12)}
         raws = {}
 
         def load_filler(r):
@@ -606,6 +604,8 @@ def tile_multiheadattention820_pa_kernel(tc, v, attn_out, dyn_w, dyn_b, out_proj
             if 0 < r < n_steps:
                 make_band(r)
             flip_filler(r)
+            if r == 1:
+                spread_bias(out_b_f32, HK // P)
             if 2 <= r < n_steps + 2:
                 flip_conv(r - 2)
                 quantise_conv(r - 2)

@@ -547,11 +547,12 @@ def tile_multiheadattention820_pa_kernel(tc, v, attn_out, dyn_w, dyn_b, out_proj
         flip_blocks(new_job(raw_d, 2, d_codes, d_scales), 0, 2)
         chunk_jobs = [chunk_job(0, raw_v0), chunk_job(1, raw_v1)]
         flip_blocks(chunk_jobs[0], 0, 2)
-        flip_blocks(chunk_jobs[1], 0, 2)
         turned = flip_psum.tile([P, P], BF16, tag="flip")
         nc.tensor.transpose(turned[:], bias_rows[:], ident_bf16[:])
         nc.scalar.copy(out=bias_columns[:], in_=turned[:, 0 : (HK + E) // P])
+        flip_blocks(chunk_jobs[1], 0, 1)
         spread_bias(dyn_b_f32, 0)
+        flip_blocks(chunk_jobs[1], 1, 1)
         logits_chunk(0, chunk_jobs[0])
         chunk_jobs.append(chunk_job(2, raw_v2))
         flip_blocks(chunk_jobs[2], 0, 2)

from contextlib import ExitStack

import concourse.mybir as mybir
from concourse.masks import make_identity

F32 = mybir.dt.float32
BF16 = mybir.dt.bfloat16
U32 = mybir.dt.uint32
U8 = mybir.dt.uint8
FP8X4 = mybir.dt.float8_e4m3fn_x4
ALU = mybir.AluOpType
ACT = mybir.ActivationFunctionType
AXIS = mybir.AxisListType

T, B, E, H, TAPS = 1024, 2, 1024, 16, 16
R = E // H
PAD_L = TAPS // 2
HK = H * TAPS

P = 128
PACK = 4
K_PASS = P * PACK
WORDS = E // 2
UNITS = 4
ROWS = UNITS * P
N_TILE = 512
TOKENS = T * B

WINDOW_STEP = P - TAPS
N_WINDOWS = (T - P) // WINDOW_STEP + 1
SWAP = PAD_L
MIDDLE_RUNS = WINDOW_STEP // TAPS

RUNS = P // TAPS
CHUNKS = [(0, 0, 2), (0, 256, 2), (0, 512, 4), (1, 0, 4), (1, 512, 4)]

LAG = TAPS - 1 - PAD_L
EDGE_ROW = 2 * TAPS


def region_words(row):
    return H * (TAPS * row + TAPS)


REGION_WORDS = [region_words(blocks * P) for b, t0, blocks in CHUNKS]
EDGE_WORDS = region_words(EDGE_ROW)
REGION_START = [sum(REGION_WORDS[:c]) + c * EDGE_WORDS for c in range(len(CHUNKS))]
EDGE_START = [REGION_START[c] + REGION_WORDS[c] for c in range(len(CHUNKS))]
SCRATCH_WORDS = EDGE_START[-1] + EDGE_WORDS + region_words(UNITS * P) // H

HEADS_PER_PASS = K_PASS // R
PAIR_HEADS = HEADS_PER_PASS
EXTRA = 2
NO_EXTRA = 4
EXTRAS = [0 if s < NO_EXTRA else EXTRA for s in range(B * N_WINDOWS)]
LIMIT_FLOPS = (2 * TOKENS * E * HK + 2 * TOKENS * (2 * E) * E) // 10
assert sum(H + PAIR_HEADS + e for e in EXTRAS) * 2 * P * P * R <= LIMIT_FLOPS
F32_HEADS = H - PAIR_HEADS
WINDOWS_AHEAD = 2
BAND_SETS = 3

FLOPS = 2 * TOKENS * E * HK + 2 * TOKENS * (2 * E) * E + 2 * TOKENS * E * TAPS


def tile_multiheadattention820_pa_kernel(tc, v, attn_out, dyn_w, dyn_b, out_proj_w, out_proj_b, out):
    nc = tc.nc
    with ExitStack() as ctx:
        consts = ctx.enter_context(tc.tile_pool(name="consts", bufs=1))
        keep = ctx.enter_context(tc.tile_pool(name="keep", bufs=1))
        raw_pool = ctx.enter_context(tc.tile_pool(name="raw", bufs=5))
        stage = ctx.enter_context(tc.tile_pool(name="stage", bufs=2))
        vq_pool = ctx.enter_context(tc.tile_pool(name="vq", bufs=2))
        soft = ctx.enter_context(tc.tile_pool(name="soft", bufs=2))
        runs_pool = ctx.enter_context(tc.tile_pool(name="runs", bufs=3))
        skew_pool = ctx.enter_context(tc.tile_pool(name="skew", bufs=2))
        win_pool = ctx.enter_context(tc.tile_pool(name="win", bufs=4))
        wide_pool = ctx.enter_context(tc.tile_pool(name="wide", bufs=3))
        conv_pool = ctx.enter_context(tc.tile_pool(name="conv", bufs=3))
        conv_q_pool = ctx.enter_context(tc.tile_pool(name="convq", bufs=2))
        out_pool = ctx.enter_context(tc.tile_pool(name="outp", bufs=3))
        flip_psum = ctx.enter_context(tc.psum_pool(name="flip", bufs=4))
        conv_psum = ctx.enter_context(tc.psum_pool(name="convp", bufs=2))
        acc_psum = ctx.enter_context(tc.psum_pool(name="acc", bufs=2))

        attn_rows = attn_out.rearrange("(n p) b c -> p n b c", p=P)
        dyn_rows = dyn_w.rearrange("(n p) c -> p n c", p=P)
        w_rows = out_proj_w.rearrange("(n p) c -> p n c", p=P)
        out_rows = out.rearrange("(n p) b e -> p n b e", p=P)
        scratch = out.rearrange("t b e -> (t b e)")[TOKENS * E - SCRATCH_WORDS : TOKENS * E]

        def load_chunk(c):
            b, t0, blocks = CHUNKS[c]
            return load_rows(v[t0 : t0 + blocks * P, b, :].rearrange("(p n) e -> p n e", n=blocks))

        def load_rows(view):
            raw = raw_pool.tile([P, UNITS * E], BF16, name="raw")
            blocks = view.shape[1]
            nc.sync.dma_start(out=raw[:, 0 : blocks * E].rearrange("p (n c) -> p n c", c=E), in_=view)
            return raw

        def load_w(nh, part):
            return load_rows(w_rows[:, nh * UNITS : (nh + 1) * UNITS, part * E : (part + 1) * E])

        def load_attn(quarter):
            b, first = quarter // 2, (quarter % 2) * UNITS
            return load_rows(attn_rows[:, first : first + UNITS, b, :])

        steps = []
        for b in range(B):
            for w in range(N_WINDOWS):
                steps.append((b, w))
        windows = {}

        def fetch_window(s):
            b, w = steps[s]
            t0 = w * WINDOW_STEP
            window_bf16 = win_pool.tile([P, E], BF16)
            nc.sync.dma_start(out=window_bf16[:], in_=v[t0 : t0 + P, b, :])
            windows[s] = window_bf16

        raw_v0 = load_chunk(0)
        raw_d = load_rows(dyn_rows)
        bias_rows = consts.tile([P, P], BF16)
        nc.vector.memset(bias_rows[:], 0.0)
        nc.sync.dma_start(out=bias_rows[0 : HK // P, :], in_=dyn_b.rearrange("(n c) -> n c", c=P))
        nc.sync.dma_start(out=bias_rows[HK // P : (HK + E) // P, :], in_=out_proj_b.rearrange("(n c) -> n c", c=P))
        raw_v1 = load_chunk(1)
        raw_v2 = load_chunk(2)
        for s in range(WINDOWS_AHEAD):
            fetch_window(s)
        raw_w = {}
        for nh in range(E // N_TILE):
            for part in range(2):
                raw_w[(nh, part)] = load_w(nh, part)
        raw_a0 = load_attn(0)

        ident_f32 = consts.tile([P, P], F32)
        make_identity(nc, ident_f32[:])

        permuted = {}
        for blocks in sorted({chunk[2] for chunk in CHUNKS}):
            perm = consts.tile([P, P], F32, name="perm%d" % blocks)
            steps_of_run = TAPS // blocks
            for m in range(steps_of_run):
                nc.vector.tensor_copy(
                    out=perm[:].rearrange("p (j m q) -> p j m q", j=blocks, q=RUNS)[:, :, m, :],
                    in_=ident_f32[:].rearrange("p (q j m) -> p j m q", q=RUNS, j=blocks)[:, :, steps_of_run - 1 - m, :],
                )
            permuted[blocks] = perm

        zeros = consts.tile([H, TAPS], F32)
        nc.vector.memset(zeros[:], 0.0)
        for (b, t0, blocks), start in zip(CHUNKS, REGION_START):
            pitch = region_words(blocks * P) // H
            ends = []
            if t0 == 0:
                ends.append(start)
            if t0 + blocks * P == T:
                ends.append(start + pitch)
            for first in ends:
                nc.sync.dma_start(
                    out=scratch[first : first + H * pitch].rearrange("(h z) -> h z", z=pitch)[:, 0:TAPS], in_=zeros[:]
                )

        warm = consts.tile([P, 1], F32)
        nc.vector.memset(warm[:], 0.0)
        nc.scalar.activation(out=warm[:], in_=warm[:], func=ACT.Exp)

        dyn_b_f32 = consts.tile([P, HK], F32)
        out_b_f32 = consts.tile([P, E], F32)
        ident_bf16 = consts.tile([P, P], BF16)
        nc.vector.tensor_copy(out=ident_bf16[:], in_=ident_f32[:])
        bias_columns = consts.tile([P, (HK + E) // P], BF16)

        reversed_f32 = consts.tile([P, P], F32)
        by_tap = reversed_f32[:].rearrange("p (h i) -> p h i", i=TAPS)
        for i in range(TAPS):
            nc.gpsimd.tensor_copy(
                out=by_tap[:, :, i : i + 1], in_=ident_f32[:].rearrange("p (h i) -> p h i", i=TAPS)[:, :, TAPS - 1 - i : TAPS - i]
            )
        reversed_bf16 = consts.tile([P, P], BF16)
        nc.vector.tensor_copy(out=reversed_bf16[:], in_=reversed_f32[:])

        band_mask = consts.tile([P, P], F32)
        nc.gpsimd.memset(band_mask[:], 1.0)
        nc.gpsimd.affine_select(
            out=band_mask[:], in_=band_mask[:], compare_op=ALU.is_ge, fill=0.0,
            base=PAD_L, pattern=[[-1, P]], channel_multiplier=1,
        )
        nc.gpsimd.affine_select(
            out=band_mask[:], in_=band_mask[:], compare_op=ALU.is_ge, fill=0.0,
            base=TAPS - 1 - PAD_L, pattern=[[1, P]], channel_multiplier=-1,
        )

        swapped_mask = consts.tile([P, P], F32)
        swapped_ident = consts.tile([P, P], F32)
        for swapped, source in ((swapped_mask, band_mask), (swapped_ident, ident_f32)):
            nc.vector.tensor_copy(out=swapped[:], in_=source[:])
            nc.vector.tensor_copy(out=swapped[:, 0:SWAP], in_=source[:, WINDOW_STEP : WINDOW_STEP + SWAP])
            nc.vector.tensor_copy(out=swapped[:, WINDOW_STEP : WINDOW_STEP + SWAP], in_=source[:, 0:SWAP])
        swapped_mask_bf16 = consts.tile([P, P], BF16)
        nc.vector.tensor_copy(out=swapped_mask_bf16[:], in_=swapped_mask[:])

        d_codes = keep.tile([P, 2 * HK], U32, align_bytes=64)
        d_scales = keep.tile([P, 2 * HK], U8, align_bytes=64)
        w_codes = keep.tile([P, 4 * E], U32, align_bytes=64)
        w_scales = keep.tile([P, 4 * E], U8, align_bytes=64)
        attn_parts = {}
        conv_parts = {}

        def new_job(raw, blocks, codes, scales, first_col=0, of_chunk=False):
            grouped = stage.tile([P, 2 * ROWS * PACK], BF16, align_bytes=64)
            return (raw, blocks, codes, scales, first_col, of_chunk, grouped)

        def flip_block(job, n):
            raw, blocks, codes, scales, first_col, of_chunk, grouped = job
            words = raw[:].bitcast(F32)
            grouped_words = grouped[:, 0 : 2 * blocks * P * PACK].bitcast(F32).rearrange("p (g r u) -> p g r u", g=2, u=2)
            flipped = flip_psum.tile([P, 4 * P], F32, tag="flip")
            order = permuted[blocks] if of_chunk else ident_f32
            for gu in range(4):
                first = n * WORDS + gu * P
                nc.tensor.transpose(flipped[:, gu * P : (gu + 1) * P], words[:, first : first + P], order[:])
            if of_chunk:
                to = grouped_words.rearrange("p g (m n q) u -> p n g m q u", m=TAPS, n=blocks)
                nc.scalar.copy(
                    out=to[:, blocks - 1 - n],
                    in_=flipped[:].rearrange("p (g u m q) -> p g m q u", g=2, u=2, m=TAPS),
                )
            else:
                nc.scalar.copy(
                    out=grouped_words[:, :, n * P : (n + 1) * P, :],
                    in_=flipped[:].rearrange("p (g u r) -> p g r u", g=2, u=2),
                )

        def quantise_job(job):
            raw, blocks, codes, scales, first_col, of_chunk, grouped = job
            cols = slice(first_col, first_col + 2 * blocks * P)
            nc.vector.quantize_mx(
                out=codes[:, cols].bitcast(FP8X4), scales=scales[:, cols], in_=grouped[:, 0 : 2 * blocks * P * PACK]
            )

        def flip_blocks(job, first, count):
            for n in range(first, first + count):
                flip_block(job, n)
            if first + count == job[1]:
                quantise_job(job)


        def chunk_job(c, raw):
            v_codes = vq_pool.tile([P, 2 * ROWS], U32, align_bytes=64)
            v_scales = vq_pool.tile([P, 2 * ROWS], U8, align_bytes=64)
            return new_job(raw, CHUNKS[c][2], v_codes, v_scales, of_chunk=True)

        exponents = {}

        def engine_of(c):
            return nc.vector if CHUNKS[c][0] == 0 else nc.gpsimd

        def logits_chunk(c, job):
            blocks = CHUNKS[c][2]
            v_codes, v_scales = job[2], job[3]
            runs = runs_pool.tile([P, UNITS * HK], F32)
            by_block = runs[:, 0 : blocks * HK].rearrange("p (h j k) -> p j h k", h=H, k=TAPS)
            for pair in range(blocks // 2):
                logits = acc_psum.tile([P, N_TILE], F32, tag="acc")
                for n in range(2):
                    for g in range(2):
                        first = (g * blocks + 2 * pair + n) * P
                        cols = slice(first, first + P)
                        nc.tensor.matmul_mx(
                            out=logits[:, n * HK : (n + 1) * HK],
                            lhsT=v_codes[:, cols].bitcast(FP8X4),
                            lhsT_scale=v_scales[:, cols],
                            rhs=d_codes[:, g * HK : (g + 1) * HK].bitcast(FP8X4),
                            rhs_scale=d_scales[:, g * HK : (g + 1) * HK],
                            start=(g == 0),
                            stop=(g == 1),
                        )
                nc.vector.tensor_tensor(
                    out=by_block[:, 2 * pair : 2 * pair + 2],
                    in0=logits[:].rearrange("p (n h k) -> p n h k", n=2, k=TAPS),
                    in1=dyn_b_f32[:].rearrange("p (h k) -> p h k", k=TAPS).unsqueeze(1).to_broadcast([P, 2, H, TAPS]),
                    op=ALU.add,
                )
            groups = blocks * H
            by_group = runs[:, 0 : blocks * HK].rearrange("p (m k) -> p m k", k=TAPS)
            top = soft.tile([P, UNITS * H], F32)
            nc.vector.tensor_reduce(out=top[:, 0:groups], in_=by_group, axis=AXIS.X, op=ALU.max)
            engine_of(c).tensor_tensor(
                out=by_group, in0=by_group, in1=top[:, 0:groups].unsqueeze(2).to_broadcast([P, groups, TAPS]), op=ALU.subtract
            )
            exponents[c] = runs

        def exponentials(c):
            wide = CHUNKS[c][2] * HK
            nc.scalar.activation(out=exponents[c][:, 0:wide], in_=exponents[c][:, 0:wide], func=ACT.Exp)

        def weights_chunk(c):
            b, t0, blocks = CHUNKS[c]
            run = blocks * TAPS
            runs = exponents[c]
            groups = blocks * H
            by_group = runs[:, 0 : blocks * HK].rearrange("p (m k) -> p m k", k=TAPS)
            total = soft.tile([P, UNITS * H], F32)
            nc.vector.tensor_reduce(out=total[:, 0:groups], in_=by_group, axis=AXIS.X, op=ALU.add)
            inverse = soft.tile([P, UNITS * H], F32)
            nc.vector.reciprocal(out=inverse[:, 0:groups], in_=total[:, 0:groups])
            engine_of(c).tensor_tensor(
                out=by_group, in0=by_group, in1=inverse[:, 0:groups].unsqueeze(2).to_broadcast([P, groups, TAPS]), op=ALU.mult
            )
            def to_scratch(start, row, parts, first, words):
                pitch = region_words(row) // H
                by_head = scratch[start : start + H * pitch].rearrange("(h z) -> h z", z=pitch)[:, TAPS:pitch]
                taps = runs[parts, 0 : blocks * HK].rearrange("p (h y) -> p h y", h=H)[:, :, words]
                each = TAPS * row // taps.shape[0]
                nc.sync.dma_start(
                    out=by_head.rearrange("h (p y) -> p h y", y=each)[:, :, first : first + taps.shape[2]], in_=taps
                )

            to_scratch(REGION_START[c], blocks * P, slice(0, P), 0, slice(0, run))
            if t0 > 0:
                to_scratch(EDGE_START[c - 1], EDGE_ROW, slice(0, P, RUNS), TAPS, slice(0, TAPS))
            if t0 + blocks * P < T:
                to_scratch(EDGE_START[c], EDGE_ROW, slice(RUNS - 1, P, RUNS), 0, slice(run - TAPS, run))

        skewed = []
        for b in range(B):
            taps_hi = keep.tile([P, T], BF16, name="hi%d" % b)
            taps_lo = keep.tile([P, T], BF16, name="lo%d" % b)
            taps_f32 = keep.tile([P, T], F32, name="taps_f32%d" % b)
            skewed.append((taps_hi, taps_lo, taps_f32))

        read_back = {}

        def read_skewed(c):
            b, t0, blocks = CHUNKS[c]
            end = t0 + blocks * P
            pieces = [(REGION_START[c], blocks * P, t0, 0 if t0 == 0 else t0 + PAD_L, T if end == T else end - PAD_L)]
            if t0 > 0:
                pieces = [(EDGE_START[c - 1], EDGE_ROW, t0 - TAPS, t0 - PAD_L, t0 + PAD_L)] + pieces
            taps_f32 = skewed[b][2]
            skew = skew_pool.tile([P, ROWS + TAPS], F32)
            first_col = pieces[0][3]
            last_col = pieces[-1][4]
            for start, row, origin, lo, hi in pieces:
                for half in range(2):
                    into = skew[:, lo - first_col : hi - first_col] if half == 0 else taps_f32[:, lo:hi]
                    first = start + half * P * (row + 1) + TAPS - LAG
                    nc.sync.dma_start(
                        out=into,
                        in_=scratch[first : first + P * (row + 1)].rearrange("(p y) -> p y", y=row + 1)[:, lo - origin : hi - origin],
                    )
            read_back[c] = (skew[:, 0 : last_col - first_col], slice(first_col, last_col))

        def split_skewed(c):
            first_heads, cols = read_back[c]
            taps_hi, taps_lo, taps_f32 = skewed[CHUNKS[c][0]]
            nc.scalar.copy(out=taps_hi[:, cols], in_=first_heads)
            nc.gpsimd.tensor_tensor(out=taps_lo[:, cols], in0=first_heads, in1=taps_hi[:, cols], op=ALU.subtract)

        wide_windows = {}
        bands = []
        for n in range(BAND_SETS):
            band_pair = keep.tile([P, 2 * PAIR_HEADS * P], BF16, name="band_pair%d" % n)
            band_extra = keep.tile([P, 2 * EXTRA * P], BF16, name="band_extra%d" % n)
            band_f32 = keep.tile([P, F32_HEADS * P], F32, name="band_f32%d" % n)
            for band in (band_pair, band_extra, band_f32):
                nc.gpsimd.memset(band[:].rearrange("p (m x) -> p m x", x=P)[:, :, WINDOW_STEP:P], 0.0)
            bands.append((band_pair, band_extra, band_f32))
        taps_x = {}
        conv_tiles = {}
        finished = {}
        grouped_conv = keep.tile([P, 2 * T * PACK], BF16, align_bytes=64)
        grouped_conv_words = grouped_conv[:].bitcast(F32).rearrange("p (g n u) -> p g n u", g=2, u=2)

        def widen_window(s):
            window_f32 = wide_pool.tile([P, F32_HEADS * R], F32)
            first = EXTRAS[s] * R
            nc.scalar.copy(out=window_f32[:, first:], in_=windows[s][:, E - F32_HEADS * R + first : E])
            wide_windows[s] = window_f32

        def banded(band, taps, mask, matrices, runs):
            shape = [P, matrices, runs, TAPS]
            nc.vector.tensor_tensor(
                out=band.rearrange("p (m a i) -> p m a i", m=matrices, i=TAPS)[:, :, 0:runs, :],
                in0=taps.rearrange("p (m i) -> p m i", i=TAPS).unsqueeze(2).to_broadcast(shape),
                in1=mask.rearrange("p (a i) -> p a i", i=TAPS)[:, 0:runs, :].unsqueeze(1).to_broadcast(shape),
                op=ALU.mult,
            )

        def make_band(s):
            b, w = steps[s]
            t0 = w * WINDOW_STEP
            taps_hi, taps_lo, taps_f32 = skewed[b]
            by_time = flip_psum.tile([P, 2 * P], F32, tag="flip")
            by_time_bf16 = by_time[:, 0:P].bitcast(BF16)
            nc.tensor.transpose(by_time_bf16[:, 0:P], taps_hi[:, t0 : t0 + P], reversed_bf16[:])
            nc.tensor.transpose(by_time_bf16[:, P : 2 * P], taps_lo[:, t0 : t0 + P], reversed_bf16[:])
            nc.tensor.transpose(by_time[:, P : 2 * P], taps_f32[:, t0 : t0 + P], reversed_f32[:])
            band_pair, band_extra, band_f32 = bands[s % BAND_SETS]
            runs = MIDDLE_RUNS if 0 < w < N_WINDOWS - 1 else P // TAPS
            extra = EXTRAS[s]
            wide = extra * TAPS
            rest = by_time[:, P : 2 * P]
            if extra > 0:
                taps_extra = wide_pool.tile([P, 2 * EXTRA * TAPS], BF16)
                nc.scalar.copy(out=taps_extra[:, 0:wide], in_=rest[:, 0:wide])
            banded(band_pair[:], by_time_bf16, swapped_mask_bf16[:], 2 * PAIR_HEADS, runs)
            if extra > 0:
                nc.vector.tensor_tensor(
                    out=taps_extra[:, wide : 2 * wide], in0=rest[:, 0:wide], in1=taps_extra[:, 0:wide], op=ALU.subtract
                )
            banded(band_f32[:, extra * P : F32_HEADS * P], rest[:, wide:P], swapped_mask[:], F32_HEADS - extra, runs)
            if extra > 0:
                banded(band_extra[:], taps_extra[:], swapped_mask_bf16[:], 2 * extra, runs)

        def start_convolution(s):
            window_bf16, window_f32 = windows[s], wide_windows[s]
            band_pair, band_extra, band_f32 = bands[s % BAND_SETS]
            extra = EXTRAS[s]
            conv_bf16 = conv_pool.tile([P, E], BF16)
            conv_tiles[s] = conv_bf16
            sums = []
            for g in range(2):
                conv_f32 = conv_psum.tile([P, K_PASS], F32, tag="conv")
                sums.append(conv_f32)
                band, in_pairs = ((band_pair, PAIR_HEADS), (band_extra, extra))[g]
                for hl in range(in_pairs):
                    h = g * HEADS_PER_PASS + hl
                    for part in range(2):
                        m = part * in_pairs + hl
                        nc.tensor.matmul(
                            out=conv_f32[:, hl * R : (hl + 1) * R],
                            lhsT=band[:, m * P : (m + 1) * P], rhs=window_bf16[:, h * R : (h + 1) * R],
                            start=(part == 0), stop=(part == 1),
                        )
                if g == 0:
                    nc.scalar.copy(out=conv_bf16[:, 0:K_PASS], in_=conv_f32[:])

            def f32_head(hl):
                nc.tensor.matmul(
                    out=sums[1][:, hl * R : (hl + 1) * R],
                    lhsT=band_f32[:, hl * P : (hl + 1) * P], rhs=window_f32[:, hl * R : (hl + 1) * R],
                    start=True, stop=True,
                )

            def finish():
                nc.scalar.copy(out=conv_bf16[:, K_PASS:E], in_=sums[1][:])

            return [lambda hl=hl: f32_head(hl) for hl in range(extra, HEADS_PER_PASS)] + [finish]

        def flip_conv(s):
            w = steps[s][1]
            t0 = w * WINDOW_STEP
            flipped_conv = flip_psum.tile([P, 4 * P], F32, tag="flip")
            conv_words = conv_tiles[s][:].bitcast(F32)
            for gu in range(4):
                nc.tensor.transpose(
                    flipped_conv[:, gu * P : (gu + 1) * P], conv_words[:, gu * P : (gu + 1) * P], swapped_ident[:]
                )
            lo = 0 if w == 0 else PAD_L
            hi = P if w == N_WINDOWS - 1 else P - PAD_L
            nc.scalar.copy(
                out=grouped_conv_words[:, :, t0 + lo : t0 + hi, :],
                in_=flipped_conv[:].rearrange("p (g u x) -> p g x u", g=2, u=2)[:, :, lo:hi, :],
            )
            first_block = 0 if w == 0 else (t0 - WINDOW_STEP + P - PAD_L) // P
            finished[s] = list(range(first_block, (t0 + hi) // P))

        def quantise_conv(s):
            b = steps[s][0]
            for block in finished[s]:
                quarter, tok = divmod(b * T + block * P, ROWS)
                if tok == 0:
                    c_codes = conv_q_pool.tile([P, 2 * ROWS], U32, align_bytes=64)
                    c_scales = conv_q_pool.tile([P, 2 * ROWS], U8, align_bytes=64)
                    conv_parts[quarter] = (c_codes, c_scales)
                c_codes, c_scales = conv_parts[quarter]
                for g in range(2):
                    first = (g * T + block * P) * PACK
                    cols = slice(g * ROWS + tok, g * ROWS + tok + P)
                    nc.vector.quantize_mx(
                        out=c_codes[:, cols].bitcast(FP8X4), scales=c_scales[:, cols], in_=grouped_conv[:, first : first + P * PACK]
                    )

        def projection(b, block):
            quarter, tok = divmod(b * T + block * P, ROWS)
            result = out_pool.tile([P, E], F32, tag="result")
            accs = {}

            def one_pass(nh, c):
                if c == 0:
                    acc = acc_psum.tile([P, N_TILE], F32, tag="acc")
                    accs[nh] = acc
                acc = accs[nh]
                codes, scales = attn_parts[quarter] if c < 2 else conv_parts[quarter]
                cols = slice((c % 2) * ROWS + tok, (c % 2) * ROWS + tok + P)
                outs = slice((nh * 4 + c) * N_TILE, (nh * 4 + c + 1) * N_TILE)
                nc.tensor.matmul_mx(
                    out=acc[:],
                    lhsT=codes[:, cols].bitcast(FP8X4),
                    lhsT_scale=scales[:, cols],
                    rhs=w_codes[:, outs].bitcast(FP8X4),
                    rhs_scale=w_scales[:, outs],
                    start=(c == 0),
                    stop=(c == 3),
                )
                if c == 3:
                    cols_out = slice(nh * N_TILE, (nh + 1) * N_TILE)
                    nc.vector.tensor_tensor(out=result[:, cols_out], in0=acc[:], in1=out_b_f32[:, cols_out], op=ALU.add)
                    if last:
                        nc.sync.dma_start(out=out_rows[:, block, b, cols_out], in_=result[:, cols_out])
                    elif nh == 1:
                        nc.sync.dma_start(out=out_rows[:, block, b, :], in_=result[:])

            last = b == B - 1 and block == T // P - 1
            return [lambda nh=nh, c=c: one_pass(nh, c) for nh in range(E // N_TILE) for c in range(4)]

        def projections(s):
            calls = []
            for block in finished[s]:
                calls = calls + projection(steps[s][0], block)
            return calls

        def w_job(nh, part, raw):
            return new_job(raw, UNITS, w_codes, w_scales, (nh * 4 + 2 * part) * N_TILE)

        def attn_job(quarter, raw_a):
            a_codes = keep.tile([P, 2 * ROWS], U32, align_bytes=64, name="a_codes%d" % quarter)
            a_scales = keep.tile([P, 2 * ROWS], U8, align_bytes=64, name="a_scales%d" % quarter)
            attn_parts[quarter] = (a_codes, a_scales)
            return new_job(raw_a, UNITS, a_codes, a_scales)

        ctx.enter_context(tc.manual_schedule(engines={mybir.EngineType.PE, mybir.EngineType.Activation}))

        jobs = {}

        def spread_bias(bias, first):
            width = bias.shape[1]
            spread = flip_psum.tile([P, E], BF16, tag="flip")
            for n in range(width // P):
                column = bias_columns[:, first + n : first + n + 1]
                nc.tensor.transpose(spread[:, n * P : (n + 1) * P], column.to_broadcast([P, P]), ident_bf16[:])
            nc.scalar.copy(out=bias[:], in_=spread[:, 0:width])

        flip_blocks(new_job(raw_d, 2, d_codes, d_scales), 0, 2)
        chunk_jobs = [chunk_job(0, raw_v0), chunk_job(1, raw_v1)]
        flip_blocks(chunk_jobs[0], 0, 2)
        turned = flip_psum.tile([P, P], BF16, tag="flip")
        nc.tensor.transpose(turned[:], bias_rows[:], ident_bf16[:])
        nc.scalar.copy(out=bias_columns[:], in_=turned[:, 0 : (HK + E) // P])
        flip_blocks(chunk_jobs[1], 0, 1)
        spread_bias(dyn_b_f32, 0)
        flip_blocks(chunk_jobs[1], 1, 1)
        logits_chunk(0, chunk_jobs[0])
        chunk_jobs.append(chunk_job(2, raw_v2))
        flip_blocks(chunk_jobs[2], 0, 2)
        logits_chunk(1, chunk_jobs[1])
        exponentials(0)
        weights_chunk(0)
        read_skewed(0)
        flip_blocks(chunk_jobs[2], 2, 2)
        exponentials(1)
        weights_chunk(1)
        read_skewed(1)
        flip_blocks(w_job(0, 0, raw_w[(0, 0)]), 0, UNITS)
        logits_chunk(2, chunk_jobs[2])
        flip_blocks(w_job(0, 1, raw_w[(0, 1)]), 0, UNITS)
        flip_blocks(w_job(1, 0, raw_w[(1, 0)]), 0, UNITS)
        split_skewed(0)
        flip_blocks(w_job(1, 1, raw_w[(1, 1)]), 0, UNITS)
        exponentials(2)
        make_band(0)
        weights_chunk(2)
        read_skewed(2)
        split_skewed(1)
        flip_blocks(attn_job(0, raw_a0), 0, UNITS)
        fillers = {
            2: ("c", 3, 0), 3: ("c", 3, 2), 4: ("a", 1, 0), 5: ("a", 1, 2), 6: ("c", 4, 0), 7: ("c", 4, 2),
            8: ("a", 2, 0), 9: ("a", 2, 2), 10: ("a", 3, 0), 11: ("a", 3, 2),
        }
        chunk_rounds = {2: (-1, -1, 3), 3: (4, 5, 8), 4: (8, 9, 12)}
        raws = {}

        def load_filler(r):
            kind, number, first = fillers.get(r, ("", 0, 1))
            if first == 0:
                raws[(kind, number)] = load_chunk(number) if kind == "c" else load_attn(number)

        def flip_filler(r):
            kind, number, first = fillers.get(r, ("", 0, 0))
            if kind != "":
                if first == 0:
                    jobs[(kind, number)] = (chunk_job if kind == "c" else attn_job)(number, raws[(kind, number)])
                flip_blocks(jobs[(kind, number)], first, 2)

        n_steps = len(steps)
        widen_window(0)
        late = []
        for r in range(n_steps + 2):
            if WINDOWS_AHEAD <= r + 1 < n_steps:
                fetch_window(r + 1)
            load_filler(r + 1)
            if 0 < r < n_steps:
                make_band(r)
            flip_filler(r)
            if r == 1:
                spread_bias(out_b_f32, HK // P)
            if 2 <= r < n_steps + 2:
                flip_conv(r - 2)
                quantise_conv(r - 2)
            for c in chunk_rounds:
                if r == chunk_rounds[c][1]:
                    exponentials(c)
                    weights_chunk(c)
                    read_skewed(c)
                if r == chunk_rounds[c][2]:
                    split_skewed(c)
            wide = []
            if 1 <= r < n_steps + 1:
                wide = start_convolution(r - 1)
            if r + 1 < n_steps:
                widen_window(r + 1)
            for c in chunk_rounds:
                if r == chunk_rounds[c][0]:
                    logits_chunk(c, jobs[("c", c)])
            passes = []
            if 3 <= r <= n_steps:
                passes = projections(r - 3)
            if r == n_steps:
                late = projections(n_steps - 2)
                passes = passes + late[0 : len(late) // 2]
            if r == n_steps + 1:
                passes = late[len(late) // 2 :] + projections(n_steps - 1)
            for n in range(max(len(wide), len(passes))):
                for calls in (wide, passes):
                    if n < len(calls):
                        calls[n]()
